import numpy as np
import ml_dtypes


def mxq(x, axis, fmt="e4m3"):
    dtype, down = {"e4m3": (ml_dtypes.float8_e4m3fn, 7), "e5m2": (ml_dtypes.float8_e5m2, 14)}[fmt]
    v = np.moveaxis(np.asarray(x, np.float32).astype(ml_dtypes.bfloat16).astype(np.float64), axis, -1)
    blocks = v.reshape(v.shape[:-1] + (-1, 32))
    amax = np.abs(blocks).max(-1, keepdims=True)
    byte = np.maximum(np.where(amax > 0, np.frexp(amax)[1] - 1 + 127, 0) - down, 1)
    scale = np.exp2(byte - 127.0)
    codes = (blocks / scale).astype(np.float32).astype(dtype).astype(np.float64)
    return np.moveaxis((codes * scale).reshape(v.shape), -1, axis)


WIDE = False


def mx_kscale(k):
    if not WIDE:
        return np.ones(k)
    levels = np.array([10, -10, 5, -5, 0])
    a = np.random.permutation(np.resize(levels, k // 512 * 4)).reshape(k // 512, 4)
    idx = np.arange(k)
    return np.exp2(a[idx // 512, idx % 128 // 32])


BF16 = ml_dtypes.bfloat16


def bf(x):
    return np.asarray(x, np.float32).astype(BF16)


def f64(x):
    return np.asarray(x).astype(np.float64)


B, N, C, DIM, H = 4, 128, 2048, 2048, 16
D = DIM // H // 2
LAYER_NUM = 12
LAM_INIT = 0.8 - 0.6 * np.exp(-0.3 * LAYER_NUM)
EPS = 1e-5


def setup_inputs():
    s = mx_kscale(C)
    sc = np.random.standard_normal((B, N, 2 * H, 2 * H))
    att = np.exp(sc) / np.exp(sc).sum(-1, keepdims=True)
    diff = att[:, :, :H, :H] - LAM_INIT * att[:, :, H:, H:]
    return {"x": bf(np.random.standard_normal((B, N, C)) * s),
            "diff": bf(diff),
            "Wv": bf(np.random.standard_normal((DIM, C)) * 0.02 * np.sqrt(H / C) / s),
            "Wo": bf(np.random.standard_normal((C, DIM)) * 2.0 / np.sqrt(DIM)),
            "bo": bf(np.random.standard_normal(C) * 0.1)}


def reference(x, diff, Wv, Wo, bo):
    v = (mxq(f64(x), 2, "e4m3") @ mxq(f64(Wv), 1, "e4m3").T).reshape(B, N, H, 2 * D)
    w = f64(diff)
    out = sum(w[:, :, :, h:h + 1] * v[:, :, h:h + 1, :] for h in range(H))
    out = out * (1.0 / np.sqrt(np.mean(out * out, axis=-1, keepdims=True) + EPS))
    out = out * (1.0 - LAM_INIT)
    out = out.reshape(B, N, DIM)
    return (mxq(out, 2, "e4m3") @ mxq(f64(Wo), 1, "e4m3").T) + f64(bo)

@@ -1,0 +1,334 @@
+import math
+
+import concourse.mybir as mybir
+from concourse.masks import make_identity
+
+F32 = mybir.dt.float32
+BF16 = mybir.dt.bfloat16
+U32 = mybir.dt.uint32
+U8 = mybir.dt.uint8
+FP8X4 = mybir.dt.float8_e4m3fn_x4
+ALU = mybir.AluOpType
+ACT = mybir.ActivationFunctionType
+AXIS = mybir.AxisListType
+
+P = 128
+PACK = 4
+K_PASS = P * PACK
+TOKENS = 512
+WIDTH = 2048
+HEADS = 16
+HEAD_COLS = WIDTH // HEADS
+PASSES = WIDTH // K_PASS
+CHUNK = 512
+CHUNKS = WIDTH // CHUNK
+ROW_TILES = CHUNK // P
+TOKEN_TILES = TOKENS // P
+GROUP_TOKENS = P // HEADS
+GROUPS = P // GROUP_TOKENS
+BANK_GROUPS = 4
+
+LAMBDA_INIT = 0.8 - 0.6 * math.exp(-0.3 * 12)
+KEEP = 1.0 - LAMBDA_INIT
+EPS = 1e-5
+
+FLOPS = 2 * 2 * TOKENS * WIDTH * WIDTH + 2 * TOKENS * HEADS * HEADS * HEAD_COLS
+
+
+RAW_BUFS = 3
+
+
+def copy_out(nc, turn, out, in_):
+    if turn % 2 == 0:
+        nc.scalar.copy(out=out, in_=in_)
+    else:
+        nc.vector.tensor_copy(out=out, in_=in_)
+
+
+def load_chunk(nc, raw_pool, rows):
+    raw = raw_pool.tile([P, ROW_TILES, WIDTH], BF16, tag="raw")
+    for r in range(ROW_TILES):
+        nc.sync.dma_start(out=raw[:, r, :], in_=rows[r * P : (r + 1) * P, :])
+    return raw
+
+
+def quantise_pass(nc, grouped, words, scales, c):
+    nc.vector.quantize_mx(out=words[:, c, :].bitcast(FP8X4), scales=scales[:, c, :], in_=grouped[:])
+
+
+def quantise_by_words(nc, pools, ident_f32, raw, words, scales):
+    raw_words = raw[:].bitcast(F32)
+    filled = None
+    for g in range(PASSES):
+        grouped = pools["grouped"].tile([P, CHUNK * PACK], BF16, align_bytes=64, tag="grouped")
+        grouped_words = grouped[:].bitcast(F32).rearrange("p (r u) -> p r u", u=2)
+        for half in range(2):
+            bank = pools["work"].tile([P, 2, 2 * P], F32, tag="work")
+            for r in range(2):
+                for u in range(2):
+                    first = (2 * g + u) * P
+                    nc.tensor.transpose(
+                        bank[:, u, r * P : (r + 1) * P],
+                        raw_words[:, 2 * half + r, first : first + P],
+                        ident_f32[:],
+                    )
+            copy_out(
+                nc,
+                half,
+                grouped_words[:, half * 2 * P : (half + 1) * 2 * P, :],
+                bank[:].rearrange("p u r -> p r u"),
+            )
+        if filled is not None:
+            quantise_pass(nc, filled, words, scales, g - 1)
+        filled = grouped
+    quantise_pass(nc, filled, words, scales, PASSES - 1)
+
+
+def quantise_by_heads(nc, pools, ident_bf16, raw, words, scales):
+    filled = None
+    for c in range(PASSES):
+        grouped = pools["grouped"].tile([P, CHUNK * PACK], BF16, align_bytes=64, tag="grouped")
+        grouped_rows = grouped[:].rearrange("p (r j) -> p r j", j=PACK)
+        for half in range(2):
+            bank = pools["work"].tile([P, PACK, 2 * P], BF16, tag="work")
+            for r in range(2):
+                for j in range(PACK):
+                    first = (PACK * c + j) * HEAD_COLS
+                    nc.tensor.transpose(
+                        bank[:, j, r * P : (r + 1) * P],
+                        raw[:, 2 * half + r, first : first + HEAD_COLS],
+                        ident_bf16[:],
+                    )
+            copy_out(
+                nc,
+                half if c < PASSES - 1 else 0,
+                grouped_rows[:, half * 2 * P : (half + 1) * 2 * P, :],
+                bank[:].rearrange("p j r -> p r j"),
+            )
+        if filled is not None:
+            quantise_pass(nc, filled, words, scales, c - 1)
+        filled = grouped
+    quantise_pass(nc, filled, words, scales, PASSES - 1)
+
+
+def product(nc, pools, lhs_words, lhs_scales, rhs_words, rhs_scales):
+    acc = pools["acc"].tile([P, CHUNK], F32, tag="acc")
+    for c in range(PASSES):
+        nc.tensor.matmul_mx(
+            out=acc[:],
+            lhsT=lhs_words[:, c, :].bitcast(FP8X4),
+            lhsT_scale=lhs_scales[:, c, :],
+            rhs=rhs_words[:, c, :].bitcast(FP8X4),
+            rhs_scale=rhs_scales[:, c, :],
+            start=(c == 0),
+            stop=(c == PASSES - 1),
+        )
+    return acc
+
+
+def tile_differentialattention_pb_kernel(tc, x, diff, Wv, Wo, bo, out):
+    nc = tc.nc
+    x_rows = x.flatten_outer_dims()
+    out_rows = out.flatten_outer_dims()
+    out_heads = out_rows.rearrange("t (h d) -> (t h) d", h=HEADS)
+    diff_rows = diff.rearrange("b n a h -> (b n a) h")
+    chunk_rows = (
+        [x_rows]
+        + [Wv[n * CHUNK : (n + 1) * CHUNK, :] for n in range(CHUNKS)]
+        + [Wo[n * CHUNK : (n + 1) * CHUNK, :] for n in range(CHUNKS)]
+    )
+
+    with (
+        tc.tile_pool(name="const", bufs=1) as const,
+        tc.tile_pool(name="raw", bufs=RAW_BUFS) as raw_pool,
+        tc.tile_pool(name="grouped", bufs=4) as grouped_pool,
+        tc.tile_pool(name="codes", bufs=CHUNKS) as codes_pool,
+        tc.tile_pool(name="staging", bufs=4) as staging,
+        tc.tile_pool(name="mixing", bufs=2) as mixing,
+        tc.tile_pool(name="parked", bufs=TOKEN_TILES) as parked,
+        tc.psum_pool(name="work", bufs=4) as work_pool,
+        tc.psum_pool(name="acc", bufs=4) as acc_pool,
+        tc.manual_schedule(),
+    ):
+        pools = {"grouped": grouped_pool, "codes": codes_pool, "work": work_pool, "acc": acc_pool}
+
+        raw_chunks = [load_chunk(nc, raw_pool, chunk_rows[k]) for k in range(RAW_BUFS)]
+        bias = const.tile([P, WIDTH], BF16)
+
+        def prepare(k, words, scales):
+            if k <= CHUNKS:
+                quantise_by_words(nc, pools, ident_f32, raw_chunks[k], words, scales)
+            else:
+                quantise_by_heads(nc, pools, ident_bf16, raw_chunks[k], words, scales)
+            if k + RAW_BUFS < len(chunk_rows):
+                raw_chunks.append(load_chunk(nc, raw_pool, chunk_rows[k + RAW_BUFS]))
+
+        def prepare_weight(k):
+            words = codes_pool.tile([P, PASSES, CHUNK], U32, align_bytes=64, tag="words")
+            scales = codes_pool.tile([P, PASSES, CHUNK], U8, align_bytes=64, tag="scales")
+            prepare(k, words, scales)
+            return words, scales
+
+        all_groups = TOKENS // GROUP_TOKENS
+        diff_ta = const.tile([P, all_groups, HEADS], BF16)
+        nc.gpsimd.dma_start(out=diff_ta[:], in_=diff_rows.rearrange("(G p) h -> p G h", p=P))
+        ident_f32 = const.tile([P, P], F32)
+        make_identity(nc, ident_f32[:])
+        ident_bf16 = const.tile([P, P], BF16)
+        make_identity(nc, ident_bf16[:])
+
+        own_half = const.tile([P, 2], F32)
+        nc.vector.tensor_reduce(
+            out=own_half[:],
+            in_=ident_f32[:].rearrange("p (q s a) -> p s q a", s=2, a=HEADS),
+            axis=AXIS.XY,
+            op=ALU.add,
+        )
+        own_quarter = const.tile([P, 4], F32)
+        nc.vector.tensor_reduce(
+            out=own_quarter[:],
+            in_=ident_f32[:].rearrange("p (q r) -> p q r", q=4),
+            axis=AXIS.X,
+            op=ALU.add,
+        )
+        pair_shape = [P, all_groups, 2, HEADS]
+        diff_pairs = const.tile([P, all_groups * 2 * HEADS], BF16, align_bytes=64)
+        nc.vector.tensor_tensor(
+            out=diff_pairs[:].rearrange("p (G s h) -> p G s h", s=2, h=HEADS),
+            in0=diff_ta[:].unsqueeze(2).to_broadcast(pair_shape),
+            in1=own_half[:].unsqueeze(1).unsqueeze(3).to_broadcast(pair_shape),
+            op=ALU.mult,
+        )
+        diff_th = const.tile([P, all_groups * 2 * HEADS], BF16, align_bytes=64)
+        nc.vector.transpose(out=diff_th[:], in_=diff_pairs[:])
+        diff_th_groups = diff_th[:].rearrange("p (G r) -> p G r", r=32)
+
+        def build_mixer(i):
+            mixer = parked.tile([P, GROUPS, P], F32, tag="mixer")
+            for q in range(4):
+                nc.scalar.activation(
+                    out=mixer[:, :, q * 32 : (q + 1) * 32],
+                    in_=diff_th_groups[:, i * GROUPS : (i + 1) * GROUPS, :],
+                    func=ACT.Copy,
+                    scale=own_quarter[:, q : q + 1],
+                )
+            return mixer
+
+        x_words = const.tile([P, PASSES, TOKENS], U32, align_bytes=64)
+        x_scales = const.tile([P, PASSES, TOKENS], U8, align_bytes=64)
+        prepare(0, x_words, x_scales)
+        next_codes = prepare_weight(1)
+        mixers = []
+        for n in range(CHUNKS):
+            wv_words, wv_scales = next_codes
+            next_codes = prepare_weight(n + 2)
+            mixers.append(build_mixer(n))
+            for i in range(TOKEN_TILES):
+                tokens = slice(i * P, (i + 1) * P)
+                acc = product(
+                    nc, pools, x_words[:, :, tokens], x_scales[:, :, tokens], wv_words, wv_scales
+                )
+                v_part = staging.tile([P, CHUNK], F32, tag="staging")
+                copy_out(nc, i, v_part[:], acc[:])
+                nc.sync.dma_start(out=out_rows[tokens, n * CHUNK : (n + 1) * CHUNK], in_=v_part[:])
+
+        v_tiles = []
+        for i in range(TOKEN_TILES):
+            v_th = parked.tile([P, GROUPS, HEAD_COLS], F32, tag="v_th")
+            nc.sync.dma_start(
+                out=v_th[:],
+                in_=out_heads[i * P * HEADS : (i + 1) * P * HEADS, :].rearrange(
+                    "(G p) d -> p G d", p=P
+                ),
+            )
+            v_tiles.append(v_th)
+        nc.sync.dma_start(out=bias[:], in_=bo.partition_broadcast(P))
+
+        wo_codes = [next_codes] + [prepare_weight(CHUNKS + 2 + n) for n in range(CHUNKS - 1)]
+
+        def mix_and_norm(i):
+            sum_sq = mixing.tile([P, GROUPS], F32)
+            rms = mixing.tile([P, GROUPS], F32)
+            gain = mixing.tile([P, GROUPS], F32)
+            r_ta = mixing.tile([P, GROUPS, HEAD_COLS], BF16)
+            for b in range(GROUPS // BANK_GROUPS):
+                in_bank = slice(b * BANK_GROUPS, (b + 1) * BANK_GROUPS)
+                mixed = work_pool.tile([P, BANK_GROUPS, HEAD_COLS], F32, tag="work")
+                for j in range(BANK_GROUPS):
+                    G = b * BANK_GROUPS + j
+                    nc.tensor.matmul(
+                        out=mixed[:, j, :],
+                        lhsT=mixers[i][:, G, :],
+                        rhs=v_tiles[i][:, G, :],
+                        start=True,
+                        stop=True,
+                    )
+                for j in range(BANK_GROUPS):
+                    G = b * BANK_GROUPS + j
+                    squares = staging.tile([P, HEAD_COLS], BF16, tag="squares")
+                    nc.scalar.activation(
+                        out=squares[:],
+                        in_=mixed[:, j, :],
+                        func=ACT.Square,
+                        accum_out=sum_sq[:, G : G + 1],
+                    )
+                nc.scalar.activation(
+                    out=rms[:, in_bank],
+                    in_=sum_sq[:, in_bank],
+                    func=ACT.Sqrt,
+                    scale=1.0 / (HEAD_COLS * KEEP * KEEP),
+                    bias=EPS / (KEEP * KEEP),
+                )
+                nc.vector.reciprocal(out=gain[:, in_bank], in_=rms[:, in_bank])
+                nc.vector.tensor_tensor(
+                    out=r_ta[:, in_bank, :],
+                    in0=mixed[:],
+                    in1=gain[:, in_bank].unsqueeze(2).to_broadcast([P, BANK_GROUPS, HEAD_COLS]),
+                    op=ALU.mult,
+                )
+            return r_ta
+
+        def transpose_and_quantise_r(r_ta):
+            r_grouped = grouped_pool.tile([P, P * HEADS], BF16, align_bytes=64, tag="grouped")
+            r_grouped_view = r_grouped[:].rearrange("p (c k j) -> p c k j", c=PASSES, j=PACK)
+            half_groups = GROUPS // 2
+            half_tokens = P // 2
+            for half in range(2):
+                r_dt = work_pool.tile([P, half_groups, P], BF16, tag="work")
+                for j in range(half_groups):
+                    nc.tensor.transpose(
+                        r_dt[:, j, :], r_ta[:, half * half_groups + j, :], ident_bf16[:]
+                    )
+                nc.scalar.copy(
+                    out=r_grouped_view[:, :, half * half_tokens : (half + 1) * half_tokens, :],
+                    in_=r_dt[:].rearrange("p G (t c j) -> p c (G t) j", c=PASSES, j=PACK),
+                )
+            r_words = mixing.tile([P, PASSES, P], U32, align_bytes=64)
+            r_scales = mixing.tile([P, PASSES, P], U8, align_bytes=64)
+            nc.vector.quantize_mx(
+                out=r_words[:].rearrange("p c k -> p (c k)").bitcast(FP8X4),
+                scales=r_scales[:].rearrange("p c k -> p (c k)"),
+                in_=r_grouped[:],
+            )
+            return r_words, r_scales
+
+        def project(i, r_words, r_scales):
+            tokens = slice(i * P, (i + 1) * P)
+            for n in range(CHUNKS):
+                wo_words, wo_scales = wo_codes[n]
+                acc = product(nc, pools, r_words, r_scales, wo_words, wo_scales)
+                out_part = staging.tile([P, CHUNK], F32, tag="staging")
+                nc.vector.tensor_tensor(
+                    out=out_part[:], in0=acc[:], in1=bias[:, n * CHUNK : (n + 1) * CHUNK], op=ALU.add
+                )
+                nc.sync.dma_start(out=out_rows[tokens, n * CHUNK : (n + 1) * CHUNK], in_=out_part[:])
+
+        r_tiles = []
+        r_codes = []
+        for step in range(TOKEN_TILES + 2):
+            if step < TOKEN_TILES:
+                r_tiles.append(mix_and_norm(step))
+            if 1 <= step <= TOKEN_TILES:
+                r_codes.append(transpose_and_quantise_r(r_tiles[step - 1]))
+            if step >= 2:
+                project(step - 2, *r_codes[step - 2])

@@ -171,7 +171,6 @@ def tile_differentialattention_pb_kernel(tc, x, diff, Wv, Wo, bo, out):
 
         all_groups = TOKENS // GROUP_TOKENS
         diff_ta = const.tile([P, all_groups, HEADS], BF16)
-        nc.gpsimd.dma_start(out=diff_ta[:], in_=diff_rows.rearrange("(G p) h -> p G h", p=P))
         ident_f32 = const.tile([P, P], F32)
         make_identity(nc, ident_f32[:])
         ident_bf16 = const.tile([P, P], BF16)
@@ -193,18 +192,11 @@ def tile_differentialattention_pb_kernel(tc, x, diff, Wv, Wo, bo, out):
         )
         pair_shape = [P, all_groups, 2, HEADS]
         diff_pairs = const.tile([P, all_groups * 2 * HEADS], BF16, align_bytes=64)
-        nc.vector.tensor_tensor(
-            out=diff_pairs[:].rearrange("p (G s h) -> p G s h", s=2, h=HEADS),
-            in0=diff_ta[:].unsqueeze(2).to_broadcast(pair_shape),
-            in1=own_half[:].unsqueeze(1).unsqueeze(3).to_broadcast(pair_shape),
-            op=ALU.mult,
-        )
         diff_th = const.tile([P, all_groups * 2 * HEADS], BF16, align_bytes=64)
-        nc.vector.transpose(out=diff_th[:], in_=diff_pairs[:])
         diff_th_groups = diff_th[:].rearrange("p (G r) -> p G r", r=32)
 
         def build_mixer(i):
-            mixer = parked.tile([P, GROUPS, P], F32, tag="mixer")
+            mixer = mixing.tile([P, GROUPS, P], F32, tag="mixer")
             for q in range(4):
                 nc.scalar.activation(
                     out=mixer[:, :, q * 32 : (q + 1) * 32],
@@ -218,11 +210,16 @@ def tile_differentialattention_pb_kernel(tc, x, diff, Wv, Wo, bo, out):
         x_scales = const.tile([P, PASSES, TOKENS], U8, align_bytes=64)
         prepare(0, x_words, x_scales)
         next_codes = prepare_weight(1)
-        mixers = []
+        nc.sync.dma_start(out=diff_ta[:], in_=diff_rows.rearrange("(G p) h -> p G h", p=P))
+        nc.gpsimd.tensor_tensor(
+            out=diff_pairs[:].rearrange("p (G s h) -> p G s h", s=2, h=HEADS),
+            in0=diff_ta[:].unsqueeze(2).to_broadcast(pair_shape),
+            in1=own_half[:].unsqueeze(1).unsqueeze(3).to_broadcast(pair_shape),
+            op=ALU.mult,
+        )
         for n in range(CHUNKS):
             wv_words, wv_scales = next_codes
             next_codes = prepare_weight(n + 2)
-            mixers.append(build_mixer(n))
             for i in range(TOKEN_TILES):
                 tokens = slice(i * P, (i + 1) * P)
                 acc = product(
@@ -243,6 +240,8 @@ def tile_differentialattention_pb_kernel(tc, x, diff, Wv, Wo, bo, out):
             )
             v_tiles.append(v_th)
         nc.sync.dma_start(out=bias[:], in_=bo.partition_broadcast(P))
+        nc.vector.transpose(out=diff_th[:], in_=diff_pairs[:])
+        mixers = [build_mixer(0)]
 
         wo_codes = [next_codes] + [prepare_weight(CHUNKS + 2 + n) for n in range(CHUNKS - 1)]
 
@@ -299,9 +298,11 @@ def tile_differentialattention_pb_kernel(tc, x, diff, Wv, Wo, bo, out):
                     nc.tensor.transpose(
                         r_dt[:, j, :], r_ta[:, half * half_groups + j, :], ident_bf16[:]
                     )
-                nc.scalar.copy(
-                    out=r_grouped_view[:, :, half * half_tokens : (half + 1) * half_tokens, :],
-                    in_=r_dt[:].rearrange("p G (t c j) -> p c (G t) j", c=PASSES, j=PACK),
+                copy_out(
+                    nc,
+                    half,
+                    r_grouped_view[:, :, half * half_tokens : (half + 1) * half_tokens, :],
+                    r_dt[:].rearrange("p G (t c j) -> p c (G t) j", c=PASSES, j=PACK),
                 )
             r_words = mixing.tile([P, PASSES, P], U32, align_bytes=64)
             r_scales = mixing.tile([P, PASSES, P], U8, align_bytes=64)
@@ -328,6 +329,8 @@ def tile_differentialattention_pb_kernel(tc, x, diff, Wv, Wo, bo, out):
         for step in range(TOKEN_TILES + 2):
             if step < TOKEN_TILES:
                 r_tiles.append(mix_and_norm(step))
+            if step + 1 < TOKEN_TILES:
+                mixers.append(build_mixer(step + 1))
             if 1 <= step <= TOKEN_TILES:
                 r_codes.append(transpose_and_quantise_r(r_tiles[step - 1]))
             if step >= 2:

@@ -26,16 +26,19 @@ ROW_TILES = CHUNK // P
 TOKEN_TILES = TOKENS // P
 GROUP_TOKENS = P // HEADS
 GROUPS = P // GROUP_TOKENS
+ALL_GROUPS = TOKENS // GROUP_TOKENS
 BANK_GROUPS = 4
+TILE_BANKS = GROUPS // BANK_GROUPS
+BANK_BF16 = 1024
+QUARTER_ROWS = P // PACK
+PSUM_BANKS = 8
+RAW_BUFS = 3
 
 LAMBDA_INIT = 0.8 - 0.6 * math.exp(-0.3 * 12)
 KEEP = 1.0 - LAMBDA_INIT
 EPS = 1e-5
 
 FLOPS = 2 * 2 * TOKENS * WIDTH * WIDTH + 2 * TOKENS * HEADS * HEADS * HEAD_COLS
-
-
-RAW_BUFS = 3
 
 
 def copy_out(nc, turn, out, in_):
@@ -45,10 +48,22 @@ def copy_out(nc, turn, out, in_):
         nc.vector.tensor_copy(out=out, in_=in_)
 
 
-def load_chunk(nc, raw_pool, rows):
+def load_rows(nc, raw_pool, rows):
     raw = raw_pool.tile([P, ROW_TILES, WIDTH], BF16, tag="raw")
     for r in range(ROW_TILES):
         nc.sync.dma_start(out=raw[:, r, :], in_=rows[r * P : (r + 1) * P, :])
+    return raw
+
+
+def load_quarters(nc, raw_pool, rows):
+    planes = CHUNK // QUARTER_ROWS
+    raw = raw_pool.tile([P, planes, K_PASS], BF16, tag="raw")
+    quarters = rows.rearrange("(R q) (j c) -> (q j) R c", q=QUARTER_ROWS, j=PACK)
+    step = planes // ROW_TILES
+    for r in range(ROW_TILES):
+        nc.sync.dma_start(
+            out=raw[:, r * step : (r + 1) * step, :], in_=quarters[:, r * step : (r + 1) * step, :]
+        )
     return raw
 
 
@@ -63,7 +78,7 @@ def quantise_by_words(nc, pools, ident_f32, raw, words, scales):
         grouped = pools["grouped"].tile([P, CHUNK * PACK], BF16, align_bytes=64, tag="grouped")
         grouped_words = grouped[:].bitcast(F32).rearrange("p (r u) -> p r u", u=2)
         for half in range(2):
-            bank = pools["work"].tile([P, 2, 2 * P], F32, tag="work")
+            bank = pools["psum"].tile([P, 2, 2 * P], F32, tag="bank")
             for r in range(2):
                 for u in range(2):
                     first = (2 * g + u) * P
@@ -84,26 +99,24 @@ def quantise_by_words(nc, pools, ident_f32, raw, words, scales):
     quantise_pass(nc, filled, words, scales, PASSES - 1)
 
 
-def quantise_by_heads(nc, pools, ident_bf16, raw, words, scales):
+def quantise_by_quarters(nc, pools, ident_bf16, raw, words, scales):
+    bank_planes = BANK_BF16 // P
     filled = None
     for c in range(PASSES):
         grouped = pools["grouped"].tile([P, CHUNK * PACK], BF16, align_bytes=64, tag="grouped")
-        grouped_rows = grouped[:].rearrange("p (r j) -> p r j", j=PACK)
         for half in range(2):
-            bank = pools["work"].tile([P, PACK, 2 * P], BF16, tag="work")
-            for r in range(2):
-                for j in range(PACK):
-                    first = (PACK * c + j) * HEAD_COLS
-                    nc.tensor.transpose(
-                        bank[:, j, r * P : (r + 1) * P],
-                        raw[:, 2 * half + r, first : first + HEAD_COLS],
-                        ident_bf16[:],
-                    )
+            bank = pools["psum"].tile([P, bank_planes, P], BF16, tag="bank")
+            for R in range(bank_planes):
+                nc.tensor.transpose(
+                    bank[:, R, :],
+                    raw[:, half * bank_planes + R, c * P : (c + 1) * P],
+                    ident_bf16[:],
+                )
             copy_out(
                 nc,
-                half if c < PASSES - 1 else 0,
-                grouped_rows[:, half * 2 * P : (half + 1) * 2 * P, :],
-                bank[:].rearrange("p j r -> p r j"),
+                1 if (2 * c + half) % 4 == 3 else 0,
+                grouped[:, half * BANK_BF16 : (half + 1) * BANK_BF16],
+                bank[:].rearrange("p R x -> p (R x)"),
             )
         if filled is not None:
             quantise_pass(nc, filled, words, scales, c - 1)
@@ -111,19 +124,16 @@ def quantise_by_heads(nc, pools, ident_bf16, raw, words, scales):
     quantise_pass(nc, filled, words, scales, PASSES - 1)
 
 
-def product(nc, pools, lhs_words, lhs_scales, rhs_words, rhs_scales):
-    acc = pools["acc"].tile([P, CHUNK], F32, tag="acc")
-    for c in range(PASSES):
-        nc.tensor.matmul_mx(
-            out=acc[:],
-            lhsT=lhs_words[:, c, :].bitcast(FP8X4),
-            lhsT_scale=lhs_scales[:, c, :],
-            rhs=rhs_words[:, c, :].bitcast(FP8X4),
-            rhs_scale=rhs_scales[:, c, :],
-            start=(c == 0),
-            stop=(c == PASSES - 1),
-        )
-    return acc
+def mx_pass(nc, acc, c, lhs_words, lhs_scales, rhs_words, rhs_scales):
+    nc.tensor.matmul_mx(
+        out=acc[:],
+        lhsT=lhs_words[:, c, :].bitcast(FP8X4),
+        lhsT_scale=lhs_scales[:, c, :],
+        rhs=rhs_words[:, c, :].bitcast(FP8X4),
+        rhs_scale=rhs_scales[:, c, :],
+        start=(c == 0),
+        stop=(c == PASSES - 1),
+    )
 
 
 def tile_differentialattention_pb_kernel(tc, x, diff, Wv, Wo, bo, out):
@@ -131,7 +141,6 @@ def tile_differentialattention_pb_kernel(tc, x, diff, Wv, Wo, bo, out):
     x_rows = x.flatten_outer_dims()
     out_rows = out.flatten_outer_dims()
     out_heads = out_rows.rearrange("t (h d) -> (t h) d", h=HEADS)
-    diff_rows = diff.rearrange("b n a h -> (b n a) h")
     chunk_rows = (
         [x_rows]
         + [Wv[n * CHUNK : (n + 1) * CHUNK, :] for n in range(CHUNKS)]
@@ -146,22 +155,25 @@ def tile_differentialattention_pb_kernel(tc, x, diff, Wv, Wo, bo, out):
         tc.tile_pool(name="staging", bufs=4) as staging,
         tc.tile_pool(name="mixing", bufs=2) as mixing,
         tc.tile_pool(name="parked", bufs=TOKEN_TILES) as parked,
-        tc.psum_pool(name="work", bufs=4) as work_pool,
-        tc.psum_pool(name="acc", bufs=4) as acc_pool,
+        tc.psum_pool(name="psum", bufs=PSUM_BANKS) as psum,
         tc.manual_schedule(),
     ):
-        pools = {"grouped": grouped_pool, "codes": codes_pool, "work": work_pool, "acc": acc_pool}
+        pools = {"grouped": grouped_pool, "psum": psum}
+        raw_chunks = []
 
-        raw_chunks = [load_chunk(nc, raw_pool, chunk_rows[k]) for k in range(RAW_BUFS)]
-        bias = const.tile([P, WIDTH], BF16)
+        def load_chunk(k):
+            if k <= CHUNKS:
+                raw_chunks.append(load_rows(nc, raw_pool, chunk_rows[k]))
+            else:
+                raw_chunks.append(load_quarters(nc, raw_pool, chunk_rows[k]))
 
         def prepare(k, words, scales):
             if k <= CHUNKS:
                 quantise_by_words(nc, pools, ident_f32, raw_chunks[k], words, scales)
             else:
-                quantise_by_heads(nc, pools, ident_bf16, raw_chunks[k], words, scales)
+                quantise_by_quarters(nc, pools, ident_bf16, raw_chunks[k], words, scales)
             if k + RAW_BUFS < len(chunk_rows):
-                raw_chunks.append(load_chunk(nc, raw_pool, chunk_rows[k + RAW_BUFS]))
+                load_chunk(k + RAW_BUFS)
 
         def prepare_weight(k):
             words = codes_pool.tile([P, PASSES, CHUNK], U32, align_bytes=64, tag="words")
@@ -169,65 +181,85 @@ def tile_differentialattention_pb_kernel(tc, x, diff, Wv, Wo, bo, out):
             prepare(k, words, scales)
             return words, scales
 
-        all_groups = TOKENS // GROUP_TOKENS
-        diff_ta = const.tile([P, all_groups, HEADS], BF16)
+        load_chunk(0)
+        half_heads = HEADS // 2
+        diff_ga = const.tile([P, GROUP_TOKENS, half_heads * HEADS], BF16)
+        diff_halves = diff.rearrange("b n a h -> (b n) (a h)").rearrange(
+            "(G t) (s c) -> s G t c", t=GROUP_TOKENS, s=2
+        )
+        for s in range(2):
+            nc.sync.dma_start(
+                out=diff_ga[s * ALL_GROUPS : (s + 1) * ALL_GROUPS, :, :], in_=diff_halves[s]
+            )
+        for k in range(1, RAW_BUFS):
+            load_chunk(k)
+
         ident_f32 = const.tile([P, P], F32)
         make_identity(nc, ident_f32[:])
         ident_bf16 = const.tile([P, P], BF16)
         make_identity(nc, ident_bf16[:])
-
-        own_half = const.tile([P, 2], F32)
+        own_token = const.tile([P, GROUP_TOKENS], F32)
         nc.vector.tensor_reduce(
-            out=own_half[:],
-            in_=ident_f32[:].rearrange("p (q s a) -> p s q a", s=2, a=HEADS),
-            axis=AXIS.XY,
-            op=ALU.add,
-        )
-        own_quarter = const.tile([P, 4], F32)
-        nc.vector.tensor_reduce(
-            out=own_quarter[:],
-            in_=ident_f32[:].rearrange("p (q r) -> p q r", q=4),
+            out=own_token[:],
+            in_=ident_f32[:].rearrange("p (t h) -> p t h", h=HEADS),
             axis=AXIS.X,
             op=ALU.add,
         )
-        pair_shape = [P, all_groups, 2, HEADS]
-        diff_pairs = const.tile([P, all_groups * 2 * HEADS], BF16, align_bytes=64)
-        diff_th = const.tile([P, all_groups * 2 * HEADS], BF16, align_bytes=64)
-        diff_th_groups = diff_th[:].rearrange("p (G r) -> p G r", r=32)
-
-        def build_mixer(i):
-            mixer = mixing.tile([P, GROUPS, P], F32, tag="mixer")
-            for q in range(4):
-                nc.scalar.activation(
-                    out=mixer[:, :, q * 32 : (q + 1) * 32],
-                    in_=diff_th_groups[:, i * GROUPS : (i + 1) * GROUPS, :],
-                    func=ACT.Copy,
-                    scale=own_quarter[:, q : q + 1],
-                )
-            return mixer
+        table_warmer = const.tile([P, 1], F32)
+        nc.scalar.activation(out=table_warmer[:], in_=own_token[:, 0:1], func=ACT.Sqrt, bias=1.0)
 
         x_words = const.tile([P, PASSES, TOKENS], U32, align_bytes=64)
         x_scales = const.tile([P, PASSES, TOKENS], U8, align_bytes=64)
         prepare(0, x_words, x_scales)
-        next_codes = prepare_weight(1)
-        nc.sync.dma_start(out=diff_ta[:], in_=diff_rows.rearrange("(G p) h -> p G h", p=P))
-        nc.gpsimd.tensor_tensor(
-            out=diff_pairs[:].rearrange("p (G s h) -> p G s h", s=2, h=HEADS),
-            in0=diff_ta[:].unsqueeze(2).to_broadcast(pair_shape),
-            in1=own_half[:].unsqueeze(1).unsqueeze(3).to_broadcast(pair_shape),
-            op=ALU.mult,
+        diff_la = const.tile([P, half_heads, P], BF16)
+        nc.scalar.copy(
+            out=diff_la[:].rearrange("p l (t h) -> p l t h", h=HEADS),
+            in_=diff_ga[:].rearrange("p t (l h) -> p l t h", h=HEADS),
         )
+        wv_codes = prepare_weight(1)
+
+        diff_th = psum.tile([P, half_heads, P], BF16, tag="bank")
+        for l in range(half_heads):
+            nc.tensor.transpose(diff_th[:, l, :], diff_la[:, l, :], ident_bf16[:])
+        weights = const.tile([P, ALL_GROUPS, PASSES, PACK], BF16)
+        for s in range(2):
+            nc.scalar.copy(
+                out=weights[:, :, :, 2 * s : 2 * s + 2],
+                in_=diff_th[:, :, s * ALL_GROUPS : (s + 1) * ALL_GROUPS].rearrange(
+                    "p (u c) G -> p G c u", u=2
+                ),
+            )
+        mixers = const.tile([P, ALL_GROUPS, P], F32)
+        mixer_columns = mixers[:].rearrange("p G (c t j) -> p G c t j", c=PASSES, j=PACK)
+
+        def build_mixer_columns(t):
+            nc.scalar.activation(
+                out=mixer_columns[:, :, :, t, :],
+                in_=weights[:],
+                func=ACT.Copy,
+                scale=own_token[:, t : t + 1],
+            )
+
         for n in range(CHUNKS):
-            wv_words, wv_scales = next_codes
-            next_codes = prepare_weight(n + 2)
+            wv_words, wv_scales = wv_codes
+            accs = [psum.tile([P, CHUNK], F32, tag="bank", name="acc") for i in range(TOKEN_TILES)]
+            for c in range(PASSES):
+                for i in range(TOKEN_TILES):
+                    tokens = slice(i * P, (i + 1) * P)
+                    mx_pass(
+                        nc, accs[i], c, x_words[:, :, tokens], x_scales[:, :, tokens],
+                        wv_words, wv_scales,
+                    )
             for i in range(TOKEN_TILES):
-                tokens = slice(i * P, (i + 1) * P)
-                acc = product(
-                    nc, pools, x_words[:, :, tokens], x_scales[:, :, tokens], wv_words, wv_scales
-                )
                 v_part = staging.tile([P, CHUNK], F32, tag="staging")
-                copy_out(nc, i, v_part[:], acc[:])
-                nc.sync.dma_start(out=out_rows[tokens, n * CHUNK : (n + 1) * CHUNK], in_=v_part[:])
+                copy_out(nc, i, v_part[:], accs[i][:])
+                nc.sync.dma_start(
+                    out=out_rows[i * P : (i + 1) * P, n * CHUNK : (n + 1) * CHUNK], in_=v_part[:]
+                )
+            if n + 1 < CHUNKS:
+                wv_codes = prepare_weight(n + 2)
+            for t in range(2 * n, 2 * n + 2):
+                build_mixer_columns(t)
 
         v_tiles = []
         for i in range(TOKEN_TILES):
@@ -239,49 +271,51 @@ def tile_differentialattention_pb_kernel(tc, x, diff, Wv, Wo, bo, out):
                 ),
             )
             v_tiles.append(v_th)
-        nc.sync.dma_start(out=bias[:], in_=bo.partition_broadcast(P))
-        nc.vector.transpose(out=diff_th[:], in_=diff_pairs[:])
-        mixers = [build_mixer(0)]
 
-        wo_codes = [next_codes] + [prepare_weight(CHUNKS + 2 + n) for n in range(CHUNKS - 1)]
+        wo_codes = [prepare_weight(CHUNKS + 1 + n) for n in range(CHUNKS - 1)]
+        bias = const.tile([P, WIDTH], BF16)
+        nc.sync.dma_start(out=bias[:], in_=bo.partition_broadcast(P))
 
         def mix_and_norm(i):
+            squares = mixing.tile([P, GROUPS, HEAD_COLS], BF16)
             sum_sq = mixing.tile([P, GROUPS], F32)
             rms = mixing.tile([P, GROUPS], F32)
             gain = mixing.tile([P, GROUPS], F32)
             r_ta = mixing.tile([P, GROUPS, HEAD_COLS], BF16)
-            for b in range(GROUPS // BANK_GROUPS):
-                in_bank = slice(b * BANK_GROUPS, (b + 1) * BANK_GROUPS)
-                mixed = work_pool.tile([P, BANK_GROUPS, HEAD_COLS], F32, tag="work")
-                for j in range(BANK_GROUPS):
-                    G = b * BANK_GROUPS + j
+            mixed_banks = []
+            for b in range(TILE_BANKS):
+                mixed = psum.tile([P, BANK_GROUPS, HEAD_COLS], F32, tag="bank")
+                mixed_banks.append(mixed)
+                for g in range(BANK_GROUPS):
+                    G = b * BANK_GROUPS + g
                     nc.tensor.matmul(
-                        out=mixed[:, j, :],
-                        lhsT=mixers[i][:, G, :],
+                        out=mixed[:, g, :],
+                        lhsT=mixers[:, i * GROUPS + G, :],
                         rhs=v_tiles[i][:, G, :],
                         start=True,
                         stop=True,
                     )
-                for j in range(BANK_GROUPS):
-                    G = b * BANK_GROUPS + j
-                    squares = staging.tile([P, HEAD_COLS], BF16, tag="squares")
+                for g in range(BANK_GROUPS):
+                    G = b * BANK_GROUPS + g
                     nc.scalar.activation(
-                        out=squares[:],
-                        in_=mixed[:, j, :],
+                        out=squares[:, G, :],
+                        in_=mixed[:, g, :],
                         func=ACT.Square,
                         accum_out=sum_sq[:, G : G + 1],
                     )
-                nc.scalar.activation(
-                    out=rms[:, in_bank],
-                    in_=sum_sq[:, in_bank],
-                    func=ACT.Sqrt,
-                    scale=1.0 / (HEAD_COLS * KEEP * KEEP),
-                    bias=EPS / (KEEP * KEEP),
-                )
-                nc.vector.reciprocal(out=gain[:, in_bank], in_=rms[:, in_bank])
+            nc.scalar.activation(
+                out=rms[:],
+                in_=sum_sq[:],
+                func=ACT.Sqrt,
+                scale=1.0 / (HEAD_COLS * KEEP * KEEP),
+                bias=EPS / (KEEP * KEEP),
+            )
+            nc.vector.reciprocal(out=gain[:], in_=rms[:])
+            for b in range(TILE_BANKS):
+                in_bank = slice(b * BANK_GROUPS, (b + 1) * BANK_GROUPS)
                 nc.vector.tensor_tensor(
                     out=r_ta[:, in_bank, :],
-                    in0=mixed[:],
+                    in0=mixed_banks[b][:],
                     in1=gain[:, in_bank].unsqueeze(2).to_broadcast([P, BANK_GROUPS, HEAD_COLS]),
                     op=ALU.mult,
                 )
@@ -289,20 +323,20 @@ def tile_differentialattention_pb_kernel(tc, x, diff, Wv, Wo, bo, out):
 
         def transpose_and_quantise_r(r_ta):
             r_grouped = grouped_pool.tile([P, P * HEADS], BF16, align_bytes=64, tag="grouped")
-            r_grouped_view = r_grouped[:].rearrange("p (c k j) -> p c k j", c=PASSES, j=PACK)
+            run = GROUP_TOKENS * PACK
+            r_grouped_view = r_grouped[:].rearrange("p (c G x) -> p c G x", c=PASSES, x=run)
             half_groups = GROUPS // 2
-            half_tokens = P // 2
             for half in range(2):
-                r_dt = work_pool.tile([P, half_groups, P], BF16, tag="work")
-                for j in range(half_groups):
+                r_dt = psum.tile([P, half_groups, P], BF16, tag="bank")
+                for g in range(half_groups):
                     nc.tensor.transpose(
-                        r_dt[:, j, :], r_ta[:, half * half_groups + j, :], ident_bf16[:]
+                        r_dt[:, g, :], r_ta[:, half * half_groups + g, :], ident_bf16[:]
                     )
                 copy_out(
                     nc,
                     half,
-                    r_grouped_view[:, :, half * half_tokens : (half + 1) * half_tokens, :],
-                    r_dt[:].rearrange("p G (t c j) -> p c (G t) j", c=PASSES, j=PACK),
+                    r_grouped_view[:, :, half * half_groups : (half + 1) * half_groups, :],
+                    r_dt[:].rearrange("p G (c x) -> p c G x", c=PASSES),
                 )
             r_words = mixing.tile([P, PASSES, P], U32, align_bytes=64)
             r_scales = mixing.tile([P, PASSES, P], U8, align_bytes=64)
@@ -317,7 +351,9 @@ def tile_differentialattention_pb_kernel(tc, x, diff, Wv, Wo, bo, out):
             tokens = slice(i * P, (i + 1) * P)
             for n in range(CHUNKS):
                 wo_words, wo_scales = wo_codes[n]
-                acc = product(nc, pools, r_words, r_scales, wo_words, wo_scales)
+                acc = psum.tile([P, CHUNK], F32, tag="bank")
+                for c in range(PASSES):
+                    mx_pass(nc, acc, c, r_words, r_scales, wo_words, wo_scales)
                 out_part = staging.tile([P, CHUNK], F32, tag="staging")
                 nc.vector.tensor_tensor(
                     out=out_part[:], in0=acc[:], in1=bias[:, n * CHUNK : (n + 1) * CHUNK], op=ALU.add
@@ -329,9 +365,9 @@ def tile_differentialattention_pb_kernel(tc, x, diff, Wv, Wo, bo, out):
         for step in range(TOKEN_TILES + 2):
             if step < TOKEN_TILES:
                 r_tiles.append(mix_and_norm(step))
-            if step + 1 < TOKEN_TILES:
-                mixers.append(build_mixer(step + 1))
             if 1 <= step <= TOKEN_TILES:
                 r_codes.append(transpose_and_quantise_r(r_tiles[step - 1]))
+            if step == 2:
+                wo_codes.append(prepare_weight(2 * CHUNKS))
             if step >= 2:
                 project(step - 2, *r_codes[step - 2])

@@ -33,6 +33,7 @@ BANK_BF16 = 1024
 QUARTER_ROWS = P // PACK
 PSUM_BANKS = 8
 RAW_BUFS = 3
+EARLY_CHUNKS = 1 + CHUNKS + 2
 
 LAMBDA_INIT = 0.8 - 0.6 * math.exp(-0.3 * 12)
 KEEP = 1.0 - LAMBDA_INIT
@@ -73,11 +74,12 @@ def quantise_pass(nc, grouped, words, scales, c):
 
 def quantise_by_words(nc, pools, ident_f32, raw, words, scales):
     raw_words = raw[:].bitcast(F32)
-    filled = None
-    for g in range(PASSES):
-        grouped = pools["grouped"].tile([P, CHUNK * PACK], BF16, align_bytes=64, tag="grouped")
-        grouped_words = grouped[:].bitcast(F32).rearrange("p (r u) -> p r u", u=2)
-        for half in range(2):
+    grouped = [
+        pools["grouped"].tile([P, CHUNK * PACK], BF16, align_bytes=64, tag="grouped", name="grouped")
+        for g in range(PASSES)
+    ]
+    for half in range(2):
+        for g in range(PASSES):
             bank = pools["psum"].tile([P, 2, 2 * P], F32, tag="bank")
             for r in range(2):
                 for u in range(2):
@@ -87,24 +89,26 @@ def quantise_by_words(nc, pools, ident_f32, raw, words, scales):
                         raw_words[:, 2 * half + r, first : first + P],
                         ident_f32[:],
                     )
+            grouped_words = grouped[g][:].bitcast(F32).rearrange("p (r u) -> p r u", u=2)
             copy_out(
                 nc,
-                half,
+                g,
                 grouped_words[:, half * 2 * P : (half + 1) * 2 * P, :],
                 bank[:].rearrange("p u r -> p r u"),
             )
-        if filled is not None:
-            quantise_pass(nc, filled, words, scales, g - 1)
-        filled = grouped
-    quantise_pass(nc, filled, words, scales, PASSES - 1)
+            if half == 1 and g >= 1:
+                quantise_pass(nc, grouped[g - 1], words, scales, g - 1)
+    quantise_pass(nc, grouped[PASSES - 1], words, scales, PASSES - 1)
 
 
 def quantise_by_quarters(nc, pools, ident_bf16, raw, words, scales):
     bank_planes = BANK_BF16 // P
-    filled = None
-    for c in range(PASSES):
-        grouped = pools["grouped"].tile([P, CHUNK * PACK], BF16, align_bytes=64, tag="grouped")
-        for half in range(2):
+    grouped = [
+        pools["grouped"].tile([P, CHUNK * PACK], BF16, align_bytes=64, tag="grouped", name="grouped")
+        for c in range(PASSES)
+    ]
+    for half in range(2):
+        for c in range(PASSES):
             bank = pools["psum"].tile([P, bank_planes, P], BF16, tag="bank")
             for R in range(bank_planes):
                 nc.tensor.transpose(
@@ -114,14 +118,13 @@ def quantise_by_quarters(nc, pools, ident_bf16, raw, words, scales):
                 )
             copy_out(
                 nc,
-                1 if (2 * c + half) % 4 == 3 else 0,
-                grouped[:, half * BANK_BF16 : (half + 1) * BANK_BF16],
+                1 if c == PASSES - 1 else 0,
+                grouped[c][:, half * BANK_BF16 : (half + 1) * BANK_BF16],
                 bank[:].rearrange("p R x -> p (R x)"),
             )
-        if filled is not None:
-            quantise_pass(nc, filled, words, scales, c - 1)
-        filled = grouped
-    quantise_pass(nc, filled, words, scales, PASSES - 1)
+            if half == 1 and c >= 1:
+                quantise_pass(nc, grouped[c - 1], words, scales, c - 1)
+    quantise_pass(nc, grouped[PASSES - 1], words, scales, PASSES - 1)
 
 
 def mx_pass(nc, acc, c, lhs_words, lhs_scales, rhs_words, rhs_scales):
@@ -172,7 +175,7 @@ def tile_differentialattention_pb_kernel(tc, x, diff, Wv, Wo, bo, out):
                 quantise_by_words(nc, pools, ident_f32, raw_chunks[k], words, scales)
             else:
                 quantise_by_quarters(nc, pools, ident_bf16, raw_chunks[k], words, scales)
-            if k + RAW_BUFS < len(chunk_rows):
+            if k + RAW_BUFS < EARLY_CHUNKS:
                 load_chunk(k + RAW_BUFS)
 
         def prepare_weight(k):
@@ -261,6 +264,7 @@ def tile_differentialattention_pb_kernel(tc, x, diff, Wv, Wo, bo, out):
             for t in range(2 * n, 2 * n + 2):
                 build_mixer_columns(t)
 
+        wo_codes = [prepare_weight(CHUNKS + 1)]
         v_tiles = []
         for i in range(TOKEN_TILES):
             v_th = parked.tile([P, GROUPS, HEAD_COLS], F32, tag="v_th")
@@ -271,10 +275,11 @@ def tile_differentialattention_pb_kernel(tc, x, diff, Wv, Wo, bo, out):
                 ),
             )
             v_tiles.append(v_th)
-
-        wo_codes = [prepare_weight(CHUNKS + 1 + n) for n in range(CHUNKS - 1)]
+            if 1 <= i and EARLY_CHUNKS + i - 1 < len(chunk_rows):
+                load_chunk(EARLY_CHUNKS + i - 1)
         bias = const.tile([P, WIDTH], BF16)
         nc.sync.dma_start(out=bias[:], in_=bo.partition_broadcast(P))
+        wo_codes.append(prepare_weight(CHUNKS + 2))
 
         def mix_and_norm(i):
             squares = mixing.tile([P, GROUPS, HEAD_COLS], BF16)
@@ -367,7 +372,7 @@ def tile_differentialattention_pb_kernel(tc, x, diff, Wv, Wo, bo, out):
                 r_tiles.append(mix_and_norm(step))
             if 1 <= step <= TOKEN_TILES:
                 r_codes.append(transpose_and_quantise_r(r_tiles[step - 1]))
-            if step == 2:
-                wo_codes.append(prepare_weight(2 * CHUNKS))
+            if 1 <= step and EARLY_CHUNKS + step - 1 < len(chunk_rows):
+                wo_codes.append(prepare_weight(EARLY_CHUNKS + step - 1))
             if step >= 2:
                 project(step - 2, *r_codes[step - 2])

@@ -33,7 +33,6 @@ BANK_BF16 = 1024
 QUARTER_ROWS = P // PACK
 PSUM_BANKS = 8
 RAW_BUFS = 3
-EARLY_CHUNKS = 1 + CHUNKS + 2
 
 LAMBDA_INIT = 0.8 - 0.6 * math.exp(-0.3 * 12)
 KEEP = 1.0 - LAMBDA_INIT
@@ -74,12 +73,11 @@ def quantise_pass(nc, grouped, words, scales, c):
 
 def quantise_by_words(nc, pools, ident_f32, raw, words, scales):
     raw_words = raw[:].bitcast(F32)
-    grouped = [
-        pools["grouped"].tile([P, CHUNK * PACK], BF16, align_bytes=64, tag="grouped", name="grouped")
-        for g in range(PASSES)
-    ]
-    for half in range(2):
-        for g in range(PASSES):
+    filled = None
+    for g in range(PASSES):
+        grouped = pools["grouped"].tile([P, CHUNK * PACK], BF16, align_bytes=64, tag="grouped")
+        grouped_words = grouped[:].bitcast(F32).rearrange("p (r u) -> p r u", u=2)
+        for half in range(2):
             bank = pools["psum"].tile([P, 2, 2 * P], F32, tag="bank")
             for r in range(2):
                 for u in range(2):
@@ -89,26 +87,24 @@ def quantise_by_words(nc, pools, ident_f32, raw, words, scales):
                         raw_words[:, 2 * half + r, first : first + P],
                         ident_f32[:],
                     )
-            grouped_words = grouped[g][:].bitcast(F32).rearrange("p (r u) -> p r u", u=2)
             copy_out(
                 nc,
-                g,
+                half,
                 grouped_words[:, half * 2 * P : (half + 1) * 2 * P, :],
                 bank[:].rearrange("p u r -> p r u"),
             )
-            if half == 1 and g >= 1:
-                quantise_pass(nc, grouped[g - 1], words, scales, g - 1)
-    quantise_pass(nc, grouped[PASSES - 1], words, scales, PASSES - 1)
+        if filled is not None:
+            quantise_pass(nc, filled, words, scales, g - 1)
+        filled = grouped
+    quantise_pass(nc, filled, words, scales, PASSES - 1)
 
 
 def quantise_by_quarters(nc, pools, ident_bf16, raw, words, scales):
     bank_planes = BANK_BF16 // P
-    grouped = [
-        pools["grouped"].tile([P, CHUNK * PACK], BF16, align_bytes=64, tag="grouped", name="grouped")
-        for c in range(PASSES)
-    ]
-    for half in range(2):
-        for c in range(PASSES):
+    filled = None
+    for c in range(PASSES):
+        grouped = pools["grouped"].tile([P, CHUNK * PACK], BF16, align_bytes=64, tag="grouped")
+        for half in range(2):
             bank = pools["psum"].tile([P, bank_planes, P], BF16, tag="bank")
             for R in range(bank_planes):
                 nc.tensor.transpose(
@@ -118,13 +114,14 @@ def quantise_by_quarters(nc, pools, ident_bf16, raw, words, scales):
                 )
             copy_out(
                 nc,
-                1 if c == PASSES - 1 else 0,
-                grouped[c][:, half * BANK_BF16 : (half + 1) * BANK_BF16],
+                half,
+                grouped[:, half * BANK_BF16 : (half + 1) * BANK_BF16],
                 bank[:].rearrange("p R x -> p (R x)"),
             )
-            if half == 1 and c >= 1:
-                quantise_pass(nc, grouped[c - 1], words, scales, c - 1)
-    quantise_pass(nc, grouped[PASSES - 1], words, scales, PASSES - 1)
+        if filled is not None:
+            quantise_pass(nc, filled, words, scales, c - 1)
+        filled = grouped
+    quantise_pass(nc, filled, words, scales, PASSES - 1)
 
 
 def mx_pass(nc, acc, c, lhs_words, lhs_scales, rhs_words, rhs_scales):
@@ -175,7 +172,7 @@ def tile_differentialattention_pb_kernel(tc, x, diff, Wv, Wo, bo, out):
                 quantise_by_words(nc, pools, ident_f32, raw_chunks[k], words, scales)
             else:
                 quantise_by_quarters(nc, pools, ident_bf16, raw_chunks[k], words, scales)
-            if k + RAW_BUFS < EARLY_CHUNKS:
+            if k + RAW_BUFS < len(chunk_rows):
                 load_chunk(k + RAW_BUFS)
 
         def prepare_weight(k):
@@ -264,7 +261,6 @@ def tile_differentialattention_pb_kernel(tc, x, diff, Wv, Wo, bo, out):
             for t in range(2 * n, 2 * n + 2):
                 build_mixer_columns(t)
 
-        wo_codes = [prepare_weight(CHUNKS + 1)]
         v_tiles = []
         for i in range(TOKEN_TILES):
             v_th = parked.tile([P, GROUPS, HEAD_COLS], F32, tag="v_th")
@@ -275,11 +271,10 @@ def tile_differentialattention_pb_kernel(tc, x, diff, Wv, Wo, bo, out):
                 ),
             )
             v_tiles.append(v_th)
-            if 1 <= i and EARLY_CHUNKS + i - 1 < len(chunk_rows):
-                load_chunk(EARLY_CHUNKS + i - 1)
+
+        wo_codes = [prepare_weight(CHUNKS + 1 + n) for n in range(CHUNKS - 1)]
         bias = const.tile([P, WIDTH], BF16)
         nc.sync.dma_start(out=bias[:], in_=bo.partition_broadcast(P))
-        wo_codes.append(prepare_weight(CHUNKS + 2))
 
         def mix_and_norm(i):
             squares = mixing.tile([P, GROUPS, HEAD_COLS], BF16)
@@ -372,7 +367,7 @@ def tile_differentialattention_pb_kernel(tc, x, diff, Wv, Wo, bo, out):
                 r_tiles.append(mix_and_norm(step))
             if 1 <= step <= TOKEN_TILES:
                 r_codes.append(transpose_and_quantise_r(r_tiles[step - 1]))
-            if 1 <= step and EARLY_CHUNKS + step - 1 < len(chunk_rows):
-                wo_codes.append(prepare_weight(EARLY_CHUNKS + step - 1))
+            if step == 2:
+                wo_codes.append(prepare_weight(2 * CHUNKS))
             if step >= 2:
                 project(step - 2, *r_codes[step - 2])

@@ -29,8 +29,7 @@ GROUPS = P // GROUP_TOKENS
 ALL_GROUPS = TOKENS // GROUP_TOKENS
 BANK_GROUPS = 4
 TILE_BANKS = GROUPS // BANK_GROUPS
-BANK_BF16 = 1024
-QUARTER_ROWS = P // PACK
+HALF = HEAD_COLS // 2
 PSUM_BANKS = 8
 RAW_BUFS = 3
 
@@ -48,30 +47,29 @@ def copy_out(nc, turn, out, in_):
         nc.vector.tensor_copy(out=out, in_=in_)
 
 
-def load_rows(nc, raw_pool, rows):
-    raw = raw_pool.tile([P, ROW_TILES, WIDTH], BF16, tag="raw")
-    for r in range(ROW_TILES):
-        nc.sync.dma_start(out=raw[:, r, :], in_=rows[r * P : (r + 1) * P, :])
-    return raw
-
-
-def load_quarters(nc, raw_pool, rows):
-    planes = CHUNK // QUARTER_ROWS
-    raw = raw_pool.tile([P, planes, K_PASS], BF16, tag="raw")
-    quarters = rows.rearrange("(R q) (j c) -> (q j) R c", q=QUARTER_ROWS, j=PACK)
-    step = planes // ROW_TILES
-    for r in range(ROW_TILES):
-        nc.sync.dma_start(
-            out=raw[:, r * step : (r + 1) * step, :], in_=quarters[:, r * step : (r + 1) * step, :]
+def transpose_row_tile(nc, pools, ident_f32, raw, r):
+    raw_words = raw[:].bitcast(F32)
+    grouped = pools["grouped"].tile([P, CHUNK * PACK], BF16, align_bytes=64, tag="grouped")
+    grouped_words = grouped[:].bitcast(F32).rearrange("p (g r u) -> p g r u", g=PASSES, u=2)
+    for half in range(2):
+        bank = pools["psum"].tile([P, 4, P], F32, tag="bank")
+        for b in range(4):
+            first = (4 * half + b) * P
+            nc.tensor.transpose(bank[:, b, :], raw_words[:, r, first : first + P], ident_f32[:])
+        copy_out(
+            nc,
+            half,
+            grouped_words[:, 2 * half : 2 * half + 2, :, :],
+            bank[:].rearrange("p (g u) r -> p g r u", u=2),
         )
-    return raw
+    return grouped
 
 
 def quantise_pass(nc, grouped, words, scales, c):
     nc.vector.quantize_mx(out=words[:, c, :].bitcast(FP8X4), scales=scales[:, c, :], in_=grouped[:])
 
 
-def quantise_by_words(nc, pools, ident_f32, raw, words, scales):
+def quantise_by_words(nc, pools, ident_f32, raw, words, scales, turns):
     raw_words = raw[:].bitcast(F32)
     filled = None
     for g in range(PASSES):
@@ -89,7 +87,7 @@ def quantise_by_words(nc, pools, ident_f32, raw, words, scales):
                     )
             copy_out(
                 nc,
-                half,
+                turns[2 * g + half],
                 grouped_words[:, half * 2 * P : (half + 1) * 2 * P, :],
                 bank[:].rearrange("p u r -> p r u"),
             )
@@ -99,41 +97,19 @@ def quantise_by_words(nc, pools, ident_f32, raw, words, scales):
     quantise_pass(nc, filled, words, scales, PASSES - 1)
 
 
-def quantise_by_quarters(nc, pools, ident_bf16, raw, words, scales):
-    bank_planes = BANK_BF16 // P
-    filled = None
+def mx_product(nc, acc, stationary, moving):
+    lhs_words, lhs_scales = stationary
+    rhs_words, rhs_scales = moving
     for c in range(PASSES):
-        grouped = pools["grouped"].tile([P, CHUNK * PACK], BF16, align_bytes=64, tag="grouped")
-        for half in range(2):
-            bank = pools["psum"].tile([P, bank_planes, P], BF16, tag="bank")
-            for R in range(bank_planes):
-                nc.tensor.transpose(
-                    bank[:, R, :],
-                    raw[:, half * bank_planes + R, c * P : (c + 1) * P],
-                    ident_bf16[:],
-                )
-            copy_out(
-                nc,
-                half,
-                grouped[:, half * BANK_BF16 : (half + 1) * BANK_BF16],
-                bank[:].rearrange("p R x -> p (R x)"),
-            )
-        if filled is not None:
-            quantise_pass(nc, filled, words, scales, c - 1)
-        filled = grouped
-    quantise_pass(nc, filled, words, scales, PASSES - 1)
-
-
-def mx_pass(nc, acc, c, lhs_words, lhs_scales, rhs_words, rhs_scales):
-    nc.tensor.matmul_mx(
-        out=acc[:],
-        lhsT=lhs_words[:, c, :].bitcast(FP8X4),
-        lhsT_scale=lhs_scales[:, c, :],
-        rhs=rhs_words[:, c, :].bitcast(FP8X4),
-        rhs_scale=rhs_scales[:, c, :],
-        start=(c == 0),
-        stop=(c == PASSES - 1),
-    )
+        nc.tensor.matmul_mx(
+            out=acc[:],
+            lhsT=lhs_words[:, c, :].bitcast(FP8X4),
+            lhsT_scale=lhs_scales[:, c, :],
+            rhs=rhs_words[:, c, :].bitcast(FP8X4),
+            rhs_scale=rhs_scales[:, c, :],
+            start=(c == 0),
+            stop=(c == PASSES - 1),
+        )
 
 
 def tile_differentialattention_pb_kernel(tc, x, diff, Wv, Wo, bo, out):
@@ -141,47 +117,41 @@ def tile_differentialattention_pb_kernel(tc, x, diff, Wv, Wo, bo, out):
     x_rows = x.flatten_outer_dims()
     out_rows = out.flatten_outer_dims()
     out_heads = out_rows.rearrange("t (h d) -> (t h) d", h=HEADS)
-    chunk_rows = (
-        [x_rows]
-        + [Wv[n * CHUNK : (n + 1) * CHUNK, :] for n in range(CHUNKS)]
-        + [Wo[n * CHUNK : (n + 1) * CHUNK, :] for n in range(CHUNKS)]
-    )
+    wv_rows = [Wv[n * CHUNK : (n + 1) * CHUNK, :] for n in range(CHUNKS)]
+    wo_rows = [Wo[n * CHUNK : (n + 1) * CHUNK, :] for n in range(CHUNKS)]
 
     with (
         tc.tile_pool(name="const", bufs=1) as const,
         tc.tile_pool(name="raw", bufs=RAW_BUFS) as raw_pool,
         tc.tile_pool(name="grouped", bufs=4) as grouped_pool,
         tc.tile_pool(name="codes", bufs=CHUNKS) as codes_pool,
-        tc.tile_pool(name="staging", bufs=4) as staging,
-        tc.tile_pool(name="mixing", bufs=2) as mixing,
+        tc.tile_pool(name="staging", bufs=8) as staging,
+        tc.tile_pool(name="mixing", bufs=6) as mixing,
         tc.tile_pool(name="parked", bufs=TOKEN_TILES) as parked,
         tc.psum_pool(name="psum", bufs=PSUM_BANKS) as psum,
         tc.manual_schedule(),
     ):
         pools = {"grouped": grouped_pool, "psum": psum}
-        raw_chunks = []
 
-        def load_chunk(k):
-            if k <= CHUNKS:
-                raw_chunks.append(load_rows(nc, raw_pool, chunk_rows[k]))
-            else:
-                raw_chunks.append(load_quarters(nc, raw_pool, chunk_rows[k]))
+        def load_rows(rows):
+            raw = raw_pool.tile([P, ROW_TILES, WIDTH], BF16, tag="raw")
+            for r in range(ROW_TILES):
+                nc.sync.dma_start(out=raw[:, r, :], in_=rows[r * P : (r + 1) * P, :])
+            return raw
 
-        def prepare(k, words, scales):
-            if k <= CHUNKS:
-                quantise_by_words(nc, pools, ident_f32, raw_chunks[k], words, scales)
-            else:
-                quantise_by_quarters(nc, pools, ident_bf16, raw_chunks[k], words, scales)
-            if k + RAW_BUFS < len(chunk_rows):
-                load_chunk(k + RAW_BUFS)
-
-        def prepare_weight(k):
+        def new_codes():
             words = codes_pool.tile([P, PASSES, CHUNK], U32, align_bytes=64, tag="words")
             scales = codes_pool.tile([P, PASSES, CHUNK], U8, align_bytes=64, tag="scales")
-            prepare(k, words, scales)
             return words, scales
 
-        load_chunk(0)
+        def prepare_weight(raw, turns):
+            codes = new_codes()
+            quantise_by_words(nc, pools, ident_f32, raw, *codes, turns)
+            return codes
+
+        wv_raw = [load_rows(wv_rows[0])]
+        x_raw = load_rows(x_rows)
+        wv_raw.append(load_rows(wv_rows[1]))
         half_heads = HEADS // 2
         diff_ga = const.tile([P, GROUP_TOKENS, half_heads * HEADS], BF16)
         diff_halves = diff.rearrange("b n a h -> (b n) (a h)").rearrange(
@@ -191,8 +161,6 @@ def tile_differentialattention_pb_kernel(tc, x, diff, Wv, Wo, bo, out):
             nc.sync.dma_start(
                 out=diff_ga[s * ALL_GROUPS : (s + 1) * ALL_GROUPS, :, :], in_=diff_halves[s]
             )
-        for k in range(1, RAW_BUFS):
-            load_chunk(k)
 
         ident_f32 = const.tile([P, P], F32)
         make_identity(nc, ident_f32[:])
@@ -205,64 +173,99 @@ def tile_differentialattention_pb_kernel(tc, x, diff, Wv, Wo, bo, out):
             axis=AXIS.X,
             op=ALU.add,
         )
+        pair_sum_f32 = const.tile([P, HALF], F32)
+        nc.vector.tensor_reduce(
+            out=pair_sum_f32[:],
+            in_=ident_f32[:].rearrange("p (n s) -> p n s", s=2),
+            axis=AXIS.X,
+            op=ALU.add,
+        )
+        pair_sum = const.tile([P, HALF], BF16)
+        nc.vector.tensor_copy(out=pair_sum[:], in_=pair_sum_f32[:])
+        parity = const.tile([P, 2], F32)
+        nc.vector.tensor_reduce(
+            out=parity[:],
+            in_=ident_f32[:].rearrange("p (n s) -> p s n", s=2),
+            axis=AXIS.X,
+            op=ALU.add,
+        )
         table_warmer = const.tile([P, 1], F32)
         nc.scalar.activation(out=table_warmer[:], in_=own_token[:, 0:1], func=ACT.Sqrt, bias=1.0)
 
-        x_words = const.tile([P, PASSES, TOKENS], U32, align_bytes=64)
-        x_scales = const.tile([P, PASSES, TOKENS], U8, align_bytes=64)
-        prepare(0, x_words, x_scales)
-        diff_la = const.tile([P, half_heads, P], BF16)
-        nc.scalar.copy(
-            out=diff_la[:].rearrange("p l (t h) -> p l t h", h=HEADS),
-            in_=diff_ga[:].rearrange("p t (l h) -> p l t h", h=HEADS),
-        )
-        wv_codes = prepare_weight(1)
+        wv_codes = [new_codes(), new_codes()]
 
-        diff_th = psum.tile([P, half_heads, P], BF16, tag="bank")
-        for l in range(half_heads):
-            nc.tensor.transpose(diff_th[:, l, :], diff_la[:, l, :], ident_bf16[:])
-        weights = const.tile([P, ALL_GROUPS, PASSES, PACK], BF16)
-        for s in range(2):
-            nc.scalar.copy(
-                out=weights[:, :, :, 2 * s : 2 * s + 2],
-                in_=diff_th[:, :, s * ALL_GROUPS : (s + 1) * ALL_GROUPS].rearrange(
-                    "p (u c) G -> p G c u", u=2
-                ),
+        def prepare_row_tile(n, r):
+            words, scales = wv_codes[n]
+            grouped = transpose_row_tile(nc, pools, ident_f32, wv_raw[n], r)
+            rows = slice(r * P, (r + 1) * P)
+            for g in range(PASSES):
+                nc.vector.quantize_mx(
+                    out=words[:, g, rows].bitcast(FP8X4),
+                    scales=scales[:, g, rows],
+                    in_=grouped[:, g * P * PACK : (g + 1) * P * PACK],
+                )
+
+        x_codes = []
+
+        def prepare_x(i):
+            grouped = transpose_row_tile(nc, pools, ident_f32, x_raw, i)
+            words = const.tile([P, PASSES, P], U32, align_bytes=64, name="x_words%d" % i)
+            scales = const.tile([P, PASSES, P], U8, align_bytes=64, name="x_scales%d" % i)
+            nc.vector.quantize_mx(
+                out=words[:].rearrange("p c k -> p (c k)").bitcast(FP8X4),
+                scales=scales[:].rearrange("p c k -> p (c k)"),
+                in_=grouped[:],
             )
+            x_codes.append((words, scales))
+
+        def multiply_v(n, i):
+            acc = psum.tile([P, CHUNK], F32, tag="bank")
+            mx_product(nc, acc, x_codes[i], wv_codes[n])
+            v_part = staging.tile([P, CHUNK], F32, tag="staging")
+            copy_out(
+                nc,
+                i,
+                v_part[:].rearrange("p (h e w) -> p h e w", e=2, w=HALF),
+                acc[:].rearrange("p (h w e) -> p h e w", e=2, w=HALF),
+            )
+            nc.sync.dma_start(
+                out=out_rows[i * P : (i + 1) * P, n * CHUNK : (n + 1) * CHUNK], in_=v_part[:]
+            )
+
         mixers = const.tile([P, ALL_GROUPS, P], F32)
-        mixer_columns = mixers[:].rearrange("p G (c t j) -> p G c t j", c=PASSES, j=PACK)
+        mixer_columns = mixers[:].rearrange("p G (g t j) -> p G g t j", g=PASSES, j=PACK)
+        weights = const.tile([P, ALL_GROUPS, HEADS], BF16)
+        diff_la = const.tile([P, half_heads, P], BF16)
+
+        def regroup_mixing_weights():
+            nc.scalar.copy(
+                out=diff_la[:].rearrange("p l (t h) -> p l t h", h=HEADS),
+                in_=diff_ga[:].rearrange("p t (l h) -> p l t h", h=HEADS),
+            )
+
+        def transpose_mixing_weights():
+            diff_th = psum.tile([P, half_heads, P], BF16, tag="bank")
+            for l in range(half_heads):
+                nc.tensor.transpose(diff_th[:, l, :], diff_la[:, l, :], ident_bf16[:])
+            for s in range(2):
+                nc.scalar.copy(
+                    out=weights[:, :, s * half_heads : (s + 1) * half_heads],
+                    in_=diff_th[:, :, s * ALL_GROUPS : (s + 1) * ALL_GROUPS].rearrange(
+                        "p l G -> p G l"
+                    ),
+                )
 
         def build_mixer_columns(t):
             nc.scalar.activation(
                 out=mixer_columns[:, :, :, t, :],
-                in_=weights[:],
+                in_=weights[:].rearrange("p G (g j) -> p G g j", j=PACK),
                 func=ACT.Copy,
                 scale=own_token[:, t : t + 1],
             )
 
-        for n in range(CHUNKS):
-            wv_words, wv_scales = wv_codes
-            accs = [psum.tile([P, CHUNK], F32, tag="bank", name="acc") for i in range(TOKEN_TILES)]
-            for c in range(PASSES):
-                for i in range(TOKEN_TILES):
-                    tokens = slice(i * P, (i + 1) * P)
-                    mx_pass(
-                        nc, accs[i], c, x_words[:, :, tokens], x_scales[:, :, tokens],
-                        wv_words, wv_scales,
-                    )
-            for i in range(TOKEN_TILES):
-                v_part = staging.tile([P, CHUNK], F32, tag="staging")
-                copy_out(nc, i, v_part[:], accs[i][:])
-                nc.sync.dma_start(
-                    out=out_rows[i * P : (i + 1) * P, n * CHUNK : (n + 1) * CHUNK], in_=v_part[:]
-                )
-            if n + 1 < CHUNKS:
-                wv_codes = prepare_weight(n + 2)
-            for t in range(2 * n, 2 * n + 2):
-                build_mixer_columns(t)
-
         v_tiles = []
-        for i in range(TOKEN_TILES):
+
+        def reload_v(i):
             v_th = parked.tile([P, GROUPS, HEAD_COLS], F32, tag="v_th")
             nc.sync.dma_start(
                 out=v_th[:],
@@ -272,37 +275,78 @@ def tile_differentialattention_pb_kernel(tc, x, diff, Wv, Wo, bo, out):
             )
             v_tiles.append(v_th)
 
-        wo_codes = [prepare_weight(CHUNKS + 1 + n) for n in range(CHUNKS - 1)]
+        BOTH = [0, 1] * 4
+        for r in range(ROW_TILES):
+            prepare_row_tile(0, r)
+        wv_raw.append(load_rows(wv_rows[2]))
+        prepare_x(0)
+        prepare_x(1)
+        multiply_v(0, 0)
+        prepare_x(2)
+        multiply_v(0, 1)
+        prepare_x(3)
+        wv_raw.append(load_rows(wv_rows[3]))
+        prepare_row_tile(1, 0)
+        multiply_v(0, 2)
+        prepare_row_tile(1, 1)
+        prepare_row_tile(1, 2)
+        prepare_row_tile(1, 3)
+        multiply_v(0, 3)
+        wo_raw = [load_rows(wo_rows[0])]
+        regroup_mixing_weights()
+        multiply_v(1, 0)
+        multiply_v(1, 1)
+        transpose_mixing_weights()
+        wv_codes.append(prepare_weight(wv_raw[2], BOTH))
+        multiply_v(1, 2)
+        build_mixer_columns(0)
+        multiply_v(1, 3)
+        build_mixer_columns(1)
+        wv_codes.append(prepare_weight(wv_raw[3], BOTH))
+        multiply_v(2, 0)
+        build_mixer_columns(2)
+        multiply_v(2, 1)
+        build_mixer_columns(3)
+        multiply_v(3, 0)
+        build_mixer_columns(4)
+        for i in range(1, TOKEN_TILES):
+            if i > 1:
+                multiply_v(2, i)
+            multiply_v(3, i)
+            reload_v(i - 1)
+            build_mixer_columns(4 + i)
+        wo_raw.append(load_rows(wo_rows[1]))
+        reload_v(3)
+        wo_raw.append(load_rows(wo_rows[2]))
         bias = const.tile([P, WIDTH], BF16)
         nc.sync.dma_start(out=bias[:], in_=bo.partition_broadcast(P))
+        wo_codes = [prepare_weight(wo_raw[0], BOTH)]
+        wo_raw.append(load_rows(wo_rows[3]))
 
-        def mix_and_norm(i):
-            squares = mixing.tile([P, GROUPS, HEAD_COLS], BF16)
-            sum_sq = mixing.tile([P, GROUPS], F32)
-            rms = mixing.tile([P, GROUPS], F32)
-            gain = mixing.tile([P, GROUPS], F32)
-            r_ta = mixing.tile([P, GROUPS, HEAD_COLS], BF16)
-            mixed_banks = []
-            for b in range(TILE_BANKS):
-                mixed = psum.tile([P, BANK_GROUPS, HEAD_COLS], F32, tag="bank")
-                mixed_banks.append(mixed)
-                for g in range(BANK_GROUPS):
-                    G = b * BANK_GROUPS + g
-                    nc.tensor.matmul(
-                        out=mixed[:, g, :],
-                        lhsT=mixers[:, i * GROUPS + G, :],
-                        rhs=v_tiles[i][:, G, :],
-                        start=True,
-                        stop=True,
-                    )
-                for g in range(BANK_GROUPS):
-                    G = b * BANK_GROUPS + g
-                    nc.scalar.activation(
-                        out=squares[:, G, :],
-                        in_=mixed[:, g, :],
-                        func=ACT.Square,
-                        accum_out=sum_sq[:, G : G + 1],
-                    )
+        squares = const.tile([P, HEAD_COLS], F32)
+        padded = {}
+
+        def mix_and_norm(k):
+            i, b = divmod(k, TILE_BANKS)
+            sum_sq = mixing.tile([P, BANK_GROUPS], F32)
+            rms = mixing.tile([P, BANK_GROUPS], F32)
+            gain = mixing.tile([P, BANK_GROUPS], F32)
+            r_bank = mixing.tile([P, BANK_GROUPS, HEAD_COLS], BF16)
+            r_padded = mixing.tile([P, 2 * BANK_GROUPS, 2, HALF], BF16)
+            mixed = psum.tile([P, BANK_GROUPS, HEAD_COLS], F32, tag="bank")
+            for g in range(BANK_GROUPS):
+                G = b * BANK_GROUPS + g
+                nc.tensor.matmul(
+                    out=mixed[:, g, :],
+                    lhsT=mixers[:, i * GROUPS + G, :],
+                    rhs=v_tiles[i][:, G, :],
+                    start=True,
+                    stop=True,
+                )
+            for g in range(BANK_GROUPS):
+                nc.scalar.activation(
+                    out=squares[:], in_=mixed[:, g, :], func=ACT.Square, accum_out=sum_sq[:, g : g + 1]
+                )
             nc.scalar.activation(
                 out=rms[:],
                 in_=sum_sq[:],
@@ -311,63 +355,99 @@ def tile_differentialattention_pb_kernel(tc, x, diff, Wv, Wo, bo, out):
                 bias=EPS / (KEEP * KEEP),
             )
             nc.vector.reciprocal(out=gain[:], in_=rms[:])
-            for b in range(TILE_BANKS):
-                in_bank = slice(b * BANK_GROUPS, (b + 1) * BANK_GROUPS)
-                nc.vector.tensor_tensor(
-                    out=r_ta[:, in_bank, :],
-                    in0=mixed_banks[b][:],
-                    in1=gain[:, in_bank].unsqueeze(2).to_broadcast([P, BANK_GROUPS, HEAD_COLS]),
-                    op=ALU.mult,
+            nc.vector.tensor_tensor(
+                out=r_bank[:],
+                in0=mixed[:],
+                in1=gain[:].unsqueeze(2).to_broadcast([P, BANK_GROUPS, HEAD_COLS]),
+                op=ALU.mult,
+            )
+            for s in range(2):
+                nc.vector.tensor_scalar(
+                    out=r_padded[:, :, s, :],
+                    in0=r_bank[:].rearrange("p G (e w) -> p (G e) w", e=2),
+                    scalar1=parity[:, s : s + 1],
+                    scalar2=None,
+                    op0=ALU.mult,
                 )
-            return r_ta
+            padded[k] = r_padded
 
-        def transpose_and_quantise_r(r_ta):
-            r_grouped = grouped_pool.tile([P, P * HEADS], BF16, align_bytes=64, tag="grouped")
-            run = GROUP_TOKENS * PACK
-            r_grouped_view = r_grouped[:].rearrange("p (c G x) -> p c G x", c=PASSES, x=run)
-            half_groups = GROUPS // 2
-            for half in range(2):
-                r_dt = psum.tile([P, half_groups, P], BF16, tag="bank")
-                for g in range(half_groups):
-                    nc.tensor.transpose(
-                        r_dt[:, g, :], r_ta[:, half * half_groups + g, :], ident_bf16[:]
+        r_grouped = {}
+        r_codes = []
+
+        def transpose_r(k, turn=0):
+            i, b = divmod(k, TILE_BANKS)
+            if b == 0:
+                fresh = grouped_pool.tile([P, CHUNK * PACK], BF16, align_bytes=64, tag="grouped")
+                r_grouped[i] = fresh
+            r_view = r_grouped[i][:].rearrange("p (g x e) -> p g x e", g=PASSES, e=2)
+            run = GROUP_TOKENS * 2
+            bank = psum.tile([P, 2, PASSES, BANK_GROUPS, run], F32, tag="bank")
+            for g in range(BANK_GROUPS):
+                for e in range(2):
+                    nc.tensor.matmul(
+                        out=bank[:, e, :, g, :],
+                        lhsT=padded[k][:, 2 * g + e, :, :].rearrange("p s w -> p (s w)"),
+                        rhs=pair_sum[:],
+                        start=True,
+                        stop=True,
                     )
-                copy_out(
-                    nc,
-                    half,
-                    r_grouped_view[:, :, half * half_groups : (half + 1) * half_groups, :],
-                    r_dt[:].rearrange("p G (c x) -> p c G x", c=PASSES),
-                )
-            r_words = mixing.tile([P, PASSES, P], U32, align_bytes=64)
-            r_scales = mixing.tile([P, PASSES, P], U8, align_bytes=64)
+            first = b * BANK_GROUPS * run
+            copy_out(
+                nc,
+                turn,
+                r_view[:, :, first : first + BANK_GROUPS * run, :],
+                bank[:].rearrange("p e g G x -> p g (G x) e"),
+            )
+
+        def quantise_r(i):
+            r_words = parked.tile([P, PASSES, P], U32, align_bytes=64)
+            r_scales = parked.tile([P, PASSES, P], U8, align_bytes=64)
             nc.vector.quantize_mx(
                 out=r_words[:].rearrange("p c k -> p (c k)").bitcast(FP8X4),
                 scales=r_scales[:].rearrange("p c k -> p (c k)"),
-                in_=r_grouped[:],
+                in_=r_grouped[i][:],
             )
-            return r_words, r_scales
+            r_codes.append((r_words, r_scales))
 
-        def project(i, r_words, r_scales):
+        def project(i, n):
             tokens = slice(i * P, (i + 1) * P)
-            for n in range(CHUNKS):
-                wo_words, wo_scales = wo_codes[n]
-                acc = psum.tile([P, CHUNK], F32, tag="bank")
-                for c in range(PASSES):
-                    mx_pass(nc, acc, c, r_words, r_scales, wo_words, wo_scales)
-                out_part = staging.tile([P, CHUNK], F32, tag="staging")
-                nc.vector.tensor_tensor(
-                    out=out_part[:], in0=acc[:], in1=bias[:, n * CHUNK : (n + 1) * CHUNK], op=ALU.add
-                )
-                nc.sync.dma_start(out=out_rows[tokens, n * CHUNK : (n + 1) * CHUNK], in_=out_part[:])
+            columns = slice(n * CHUNK, (n + 1) * CHUNK)
+            acc = psum.tile([P, CHUNK], F32, tag="bank")
+            mx_product(nc, acc, r_codes[i], wo_codes[n])
+            out_part = staging.tile([P, CHUNK], F32, tag="staging")
+            nc.vector.tensor_tensor(out=out_part[:], in0=acc[:], in1=bias[:, columns], op=ALU.add)
+            nc.sync.dma_start(out=out_rows[tokens, columns], in_=out_part[:])
 
-        r_tiles = []
-        r_codes = []
-        for step in range(TOKEN_TILES + 2):
-            if step < TOKEN_TILES:
-                r_tiles.append(mix_and_norm(step))
-            if 1 <= step <= TOKEN_TILES:
-                r_codes.append(transpose_and_quantise_r(r_tiles[step - 1]))
-            if step == 2:
-                wo_codes.append(prepare_weight(2 * CHUNKS))
-            if step >= 2:
-                project(step - 2, *r_codes[step - 2])
+        MOST = [0, 0, 1, 0, 0, 1, 0, 1]
+        LAG = 3
+        def mix_tile(i):
+            for k in range(TILE_BANKS * i, TILE_BANKS * (i + 1)):
+                mix_and_norm(k)
+                if k >= LAG:
+                    transpose_r(k - LAG, 1 if k % 4 == 0 else 0)
+                    if (k - LAG) % TILE_BANKS == TILE_BANKS - 1:
+                        quantise_r((k - LAG) // TILE_BANKS)
+
+        mix_tile(0)
+        mix_tile(1)
+        wo_codes.append(prepare_weight(wo_raw[1], MOST))
+        mix_tile(2)
+        project(0, 0)
+        project(0, 1)
+        project(1, 0)
+        wo_codes.append(prepare_weight(wo_raw[2], MOST))
+        project(1, 1)
+        mix_tile(3)
+        project(0, 2)
+        project(1, 2)
+        for k in range(16 - LAG, 16):
+            transpose_r(k)
+        project(2, 0)
+        quantise_r(3)
+        project(2, 1)
+        project(2, 2)
+        wo_codes.append(prepare_weight(wo_raw[3], MOST))
+        for n in range(CHUNKS - 1):
+            project(3, n)
+        for i in range(TOKEN_TILES):
+            project(i, 3)

@@ -31,6 +31,8 @@ BANK_GROUPS = 4
 TILE_BANKS = GROUPS // BANK_GROUPS
 HALF = HEAD_COLS // 2
 PSUM_BANKS = 8
+RT = ((0, 0), (0, 0), (0, 0))
+VT = ((1, 1, 1, 1),) + ((0, 1, 0, 1),) * 3
 RAW_BUFS = 3
 
 LAMBDA_INIT = 0.8 - 0.6 * math.exp(-0.3 * 12)
@@ -47,7 +49,7 @@ def copy_out(nc, turn, out, in_):
         nc.vector.tensor_copy(out=out, in_=in_)
 
 
-def transpose_row_tile(nc, pools, ident_f32, raw, r):
+def transpose_row_tile(nc, pools, ident_f32, raw, r, turns):
     raw_words = raw[:].bitcast(F32)
     grouped = pools["grouped"].tile([P, CHUNK * PACK], BF16, align_bytes=64, tag="grouped")
     grouped_words = grouped[:].bitcast(F32).rearrange("p (g r u) -> p g r u", g=PASSES, u=2)
@@ -58,43 +60,34 @@ def transpose_row_tile(nc, pools, ident_f32, raw, r):
             nc.tensor.transpose(bank[:, b, :], raw_words[:, r, first : first + P], ident_f32[:])
         copy_out(
             nc,
-            half,
+            turns[half],
             grouped_words[:, 2 * half : 2 * half + 2, :, :],
             bank[:].rearrange("p (g u) r -> p g r u", u=2),
         )
     return grouped
 
 
-def quantise_pass(nc, grouped, words, scales, c):
-    nc.vector.quantize_mx(out=words[:, c, :].bitcast(FP8X4), scales=scales[:, c, :], in_=grouped[:])
-
-
-def quantise_by_words(nc, pools, ident_f32, raw, words, scales, turns):
+def transpose_pass(nc, pools, ident_f32, raw, g, turns):
     raw_words = raw[:].bitcast(F32)
-    filled = None
-    for g in range(PASSES):
-        grouped = pools["grouped"].tile([P, CHUNK * PACK], BF16, align_bytes=64, tag="grouped")
-        grouped_words = grouped[:].bitcast(F32).rearrange("p (r u) -> p r u", u=2)
-        for half in range(2):
-            bank = pools["psum"].tile([P, 2, 2 * P], F32, tag="bank")
-            for r in range(2):
-                for u in range(2):
-                    first = (2 * g + u) * P
-                    nc.tensor.transpose(
-                        bank[:, u, r * P : (r + 1) * P],
-                        raw_words[:, 2 * half + r, first : first + P],
-                        ident_f32[:],
-                    )
-            copy_out(
-                nc,
-                turns[2 * g + half],
-                grouped_words[:, half * 2 * P : (half + 1) * 2 * P, :],
-                bank[:].rearrange("p u r -> p r u"),
-            )
-        if filled is not None:
-            quantise_pass(nc, filled, words, scales, g - 1)
-        filled = grouped
-    quantise_pass(nc, filled, words, scales, PASSES - 1)
+    grouped = pools["grouped"].tile([P, CHUNK * PACK], BF16, align_bytes=64, tag="grouped")
+    grouped_words = grouped[:].bitcast(F32).rearrange("p (r u) -> p r u", u=2)
+    for half in range(2):
+        bank = pools["psum"].tile([P, 2, 2 * P], F32, tag="bank")
+        for r in range(2):
+            for u in range(2):
+                first = (2 * g + u) * P
+                nc.tensor.transpose(
+                    bank[:, u, r * P : (r + 1) * P],
+                    raw_words[:, 2 * half + r, first : first + P],
+                    ident_f32[:],
+                )
+        copy_out(
+            nc,
+            turns[half],
+            grouped_words[:, half * 2 * P : (half + 1) * 2 * P, :],
+            bank[:].rearrange("p u r -> p r u"),
+        )
+    return grouped
 
 
 def mx_product(nc, acc, stationary, moving):
@@ -126,17 +119,19 @@ def tile_differentialattention_pb_kernel(tc, x, diff, Wv, Wo, bo, out):
         tc.tile_pool(name="grouped", bufs=4) as grouped_pool,
         tc.tile_pool(name="codes", bufs=CHUNKS) as codes_pool,
         tc.tile_pool(name="staging", bufs=8) as staging,
-        tc.tile_pool(name="mixing", bufs=6) as mixing,
+        tc.tile_pool(name="mixing", bufs=4) as mixing,
         tc.tile_pool(name="parked", bufs=TOKEN_TILES) as parked,
         tc.psum_pool(name="psum", bufs=PSUM_BANKS) as psum,
         tc.manual_schedule(),
     ):
         pools = {"grouped": grouped_pool, "psum": psum}
 
-        def load_rows(rows):
+        def load_rows(rows, pieces):
             raw = raw_pool.tile([P, ROW_TILES, WIDTH], BF16, tag="raw")
-            for r in range(ROW_TILES):
-                nc.sync.dma_start(out=raw[:, r, :], in_=rows[r * P : (r + 1) * P, :])
+            planes = ROW_TILES // pieces
+            by_plane = rows.rearrange("(r p) k -> p r k", p=P)
+            for r in range(0, ROW_TILES, planes):
+                nc.sync.dma_start(out=raw[:, r : r + planes, :], in_=by_plane[:, r : r + planes, :])
             return raw
 
         def new_codes():
@@ -144,14 +139,30 @@ def tile_differentialattention_pb_kernel(tc, x, diff, Wv, Wo, bo, out):
             scales = codes_pool.tile([P, PASSES, CHUNK], U8, align_bytes=64, tag="scales")
             return words, scales
 
-        def prepare_weight(raw, turns):
+        waiting = []
+
+        def quantise_waiting():
+            if waiting:
+                grouped, (words, scales), g = waiting.pop()
+                nc.vector.quantize_mx(
+                    out=words[:, g, :].bitcast(FP8X4), scales=scales[:, g, :], in_=grouped[:]
+                )
+
+        def prepare_pass(raw, codes, g, turns=(0, 1)):
+            grouped = transpose_pass(nc, pools, ident_f32, raw, g, turns)
+            quantise_waiting()
+            waiting.append((grouped, codes, g))
+
+        def prepare_weight(raw, turns=((0, 1),) * PASSES):
             codes = new_codes()
-            quantise_by_words(nc, pools, ident_f32, raw, *codes, turns)
+            for g in range(PASSES):
+                prepare_pass(raw, codes, g, turns[g])
+            quantise_waiting()
             return codes
 
-        wv_raw = [load_rows(wv_rows[0])]
-        x_raw = load_rows(x_rows)
-        wv_raw.append(load_rows(wv_rows[1]))
+        wv_raw = [load_rows(wv_rows[0], 4)]
+        x_raw = load_rows(x_rows, 4)
+        wv_raw.append(load_rows(wv_rows[1], 4))
         half_heads = HEADS // 2
         diff_ga = const.tile([P, GROUP_TOKENS, half_heads * HEADS], BF16)
         diff_halves = diff.rearrange("b n a h -> (b n) (a h)").rearrange(
@@ -196,7 +207,7 @@ def tile_differentialattention_pb_kernel(tc, x, diff, Wv, Wo, bo, out):
 
         def prepare_row_tile(n, r):
             words, scales = wv_codes[n]
-            grouped = transpose_row_tile(nc, pools, ident_f32, wv_raw[n], r)
+            grouped = transpose_row_tile(nc, pools, ident_f32, wv_raw[n], r, RT[n])
             rows = slice(r * P, (r + 1) * P)
             for g in range(PASSES):
                 nc.vector.quantize_mx(
@@ -208,7 +219,7 @@ def tile_differentialattention_pb_kernel(tc, x, diff, Wv, Wo, bo, out):
         x_codes = []
 
         def prepare_x(i):
-            grouped = transpose_row_tile(nc, pools, ident_f32, x_raw, i)
+            grouped = transpose_row_tile(nc, pools, ident_f32, x_raw, i, RT[2])
             words = const.tile([P, PASSES, P], U32, align_bytes=64, name="x_words%d" % i)
             scales = const.tile([P, PASSES, P], U8, align_bytes=64, name="x_scales%d" % i)
             nc.vector.quantize_mx(
@@ -224,7 +235,7 @@ def tile_differentialattention_pb_kernel(tc, x, diff, Wv, Wo, bo, out):
             v_part = staging.tile([P, CHUNK], F32, tag="staging")
             copy_out(
                 nc,
-                i,
+                VT[n][i],
                 v_part[:].rearrange("p (h e w) -> p h e w", e=2, w=HALF),
                 acc[:].rearrange("p (h w e) -> p h e w", e=2, w=HALF),
             )
@@ -275,34 +286,34 @@ def tile_differentialattention_pb_kernel(tc, x, diff, Wv, Wo, bo, out):
             )
             v_tiles.append(v_th)
 
-        BOTH = [0, 1] * 4
         for r in range(ROW_TILES):
             prepare_row_tile(0, r)
-        wv_raw.append(load_rows(wv_rows[2]))
+        wv_raw.append(load_rows(wv_rows[2], 2))
         prepare_x(0)
         prepare_x(1)
         multiply_v(0, 0)
         prepare_x(2)
         multiply_v(0, 1)
         prepare_x(3)
-        wv_raw.append(load_rows(wv_rows[3]))
+        wv_raw.append(load_rows(wv_rows[3], 2))
         prepare_row_tile(1, 0)
         multiply_v(0, 2)
         prepare_row_tile(1, 1)
         prepare_row_tile(1, 2)
         prepare_row_tile(1, 3)
         multiply_v(0, 3)
-        wo_raw = [load_rows(wo_rows[0])]
+        wo_raw = [load_rows(wo_rows[0], 2)]
         regroup_mixing_weights()
         multiply_v(1, 0)
         multiply_v(1, 1)
         transpose_mixing_weights()
-        wv_codes.append(prepare_weight(wv_raw[2], BOTH))
+        wv_codes.append(prepare_weight(wv_raw[2]))
+        wo_raw.append(load_rows(wo_rows[1], 2))
         multiply_v(1, 2)
         build_mixer_columns(0)
         multiply_v(1, 3)
         build_mixer_columns(1)
-        wv_codes.append(prepare_weight(wv_raw[3], BOTH))
+        wv_codes.append(prepare_weight(wv_raw[3]))
         multiply_v(2, 0)
         build_mixer_columns(2)
         multiply_v(2, 1)
@@ -314,26 +325,24 @@ def tile_differentialattention_pb_kernel(tc, x, diff, Wv, Wo, bo, out):
                 multiply_v(2, i)
             multiply_v(3, i)
             reload_v(i - 1)
+            if i == 2:
+                wo_raw.append(load_rows(wo_rows[2], 2))
             build_mixer_columns(4 + i)
-        wo_raw.append(load_rows(wo_rows[1]))
         reload_v(3)
-        wo_raw.append(load_rows(wo_rows[2]))
         bias = const.tile([P, WIDTH], BF16)
         nc.sync.dma_start(out=bias[:], in_=bo.partition_broadcast(P))
-        wo_codes = [prepare_weight(wo_raw[0], BOTH)]
-        wo_raw.append(load_rows(wo_rows[3]))
+        wo_codes = [prepare_weight(wo_raw[0])]
+        wo_raw.append(load_rows(wo_rows[3], 2))
+        wo_codes.append(prepare_weight(wo_raw[1], ((0, 0), (0, 1), (0, 0), (0, 1))))
 
-        squares = const.tile([P, HEAD_COLS], F32)
-        padded = {}
 
-        def mix_and_norm(k):
+        live = {}
+
+        def mix(k):
             i, b = divmod(k, TILE_BANKS)
-            sum_sq = mixing.tile([P, BANK_GROUPS], F32)
-            rms = mixing.tile([P, BANK_GROUPS], F32)
-            gain = mixing.tile([P, BANK_GROUPS], F32)
-            r_bank = mixing.tile([P, BANK_GROUPS, HEAD_COLS], BF16)
-            r_padded = mixing.tile([P, 2 * BANK_GROUPS, 2, HALF], BF16)
             mixed = psum.tile([P, BANK_GROUPS, HEAD_COLS], F32, tag="bank")
+            sum_sq = mixing.tile([P, BANK_GROUPS], F32)
+            squares = mixing.tile([P, BANK_GROUPS, HEAD_COLS], BF16)
             for g in range(BANK_GROUPS):
                 G = b * BANK_GROUPS + g
                 nc.tensor.matmul(
@@ -345,31 +354,46 @@ def tile_differentialattention_pb_kernel(tc, x, diff, Wv, Wo, bo, out):
                 )
             for g in range(BANK_GROUPS):
                 nc.scalar.activation(
-                    out=squares[:], in_=mixed[:, g, :], func=ACT.Square, accum_out=sum_sq[:, g : g + 1]
+                    out=squares[:, g, :], in_=mixed[:, g, :], func=ACT.Square, accum_out=sum_sq[:, g : g + 1]
                 )
-            nc.scalar.activation(
-                out=rms[:],
-                in_=sum_sq[:],
-                func=ACT.Sqrt,
-                scale=1.0 / (HEAD_COLS * KEEP * KEEP),
-                bias=EPS / (KEEP * KEEP),
-            )
-            nc.vector.reciprocal(out=gain[:], in_=rms[:])
-            nc.vector.tensor_tensor(
-                out=r_bank[:],
-                in0=mixed[:],
-                in1=gain[:].unsqueeze(2).to_broadcast([P, BANK_GROUPS, HEAD_COLS]),
-                op=ALU.mult,
-            )
+            live["mixed", k] = mixed
+            live["sum_sq", k] = sum_sq
+
+        def normalise(k):
+            rms = mixing.tile([P, BANK_GROUPS], F32)
+            gain = mixing.tile([P, BANK_GROUPS], F32)
+            r_bank = mixing.tile([P, BANK_GROUPS, HEAD_COLS], BF16)
+            if k < 16:
+                nc.scalar.activation(
+                    out=rms[:],
+                    in_=live["sum_sq", k][:],
+                    func=ACT.Sqrt,
+                    scale=1.0 / (HEAD_COLS * KEEP * KEEP),
+                    bias=EPS / (KEEP * KEEP),
+                )
+                nc.vector.reciprocal(out=gain[:], in_=rms[:])
+            if k >= MASK_LAG:
+                pad(k - MASK_LAG)
+            if k < 16:
+                nc.vector.tensor_tensor(
+                    out=r_bank[:],
+                    in0=live["mixed", k][:],
+                    in1=gain[:].unsqueeze(2).to_broadcast([P, BANK_GROUPS, HEAD_COLS]),
+                    op=ALU.mult,
+                )
+                live["r", k] = r_bank
+
+        def pad(k):
+            r_padded = mixing.tile([P, 2 * BANK_GROUPS, 2, HALF], BF16)
             for s in range(2):
                 nc.vector.tensor_scalar(
                     out=r_padded[:, :, s, :],
-                    in0=r_bank[:].rearrange("p G (e w) -> p (G e) w", e=2),
+                    in0=live["r", k][:].rearrange("p G (e w) -> p (G e) w", e=2),
                     scalar1=parity[:, s : s + 1],
                     scalar2=None,
                     op0=ALU.mult,
                 )
-            padded[k] = r_padded
+            live["padded", k] = r_padded
 
         r_grouped = {}
         r_codes = []
@@ -386,7 +410,7 @@ def tile_differentialattention_pb_kernel(tc, x, diff, Wv, Wo, bo, out):
                 for e in range(2):
                     nc.tensor.matmul(
                         out=bank[:, e, :, g, :],
-                        lhsT=padded[k][:, 2 * g + e, :, :].rearrange("p s w -> p (s w)"),
+                        lhsT=live["padded", k][:, 2 * g + e, :, :].rearrange("p s w -> p (s w)"),
                         rhs=pair_sum[:],
                         start=True,
                         stop=True,
@@ -418,36 +442,36 @@ def tile_differentialattention_pb_kernel(tc, x, diff, Wv, Wo, bo, out):
             nc.vector.tensor_tensor(out=out_part[:], in0=acc[:], in1=bias[:, columns], op=ALU.add)
             nc.sync.dma_start(out=out_rows[tokens, columns], in_=out_part[:])
 
-        MOST = [0, 0, 1, 0, 0, 1, 0, 1]
-        LAG = 3
-        def mix_tile(i):
-            for k in range(TILE_BANKS * i, TILE_BANKS * (i + 1)):
-                mix_and_norm(k)
-                if k >= LAG:
-                    transpose_r(k - LAG, 1 if k % 4 == 0 else 0)
-                    if (k - LAG) % TILE_BANKS == TILE_BANKS - 1:
-                        quantise_r((k - LAG) // TILE_BANKS)
+        LAG = 4
+        MASK_LAG = 2
 
-        mix_tile(0)
-        mix_tile(1)
-        wo_codes.append(prepare_weight(wo_raw[1], MOST))
-        mix_tile(2)
-        project(0, 0)
-        project(0, 1)
-        project(1, 0)
-        wo_codes.append(prepare_weight(wo_raw[2], MOST))
-        project(1, 1)
-        mix_tile(3)
-        project(0, 2)
-        project(1, 2)
-        for k in range(16 - LAG, 16):
-            transpose_r(k)
-        project(2, 0)
-        quantise_r(3)
-        project(2, 1)
-        project(2, 2)
-        wo_codes.append(prepare_weight(wo_raw[3], MOST))
-        for n in range(CHUNKS - 1):
-            project(3, n)
-        for i in range(TOKEN_TILES):
+        def tick(k):
+            if k < 16:
+                mix(k)
+            if LAG <= k < 16 + LAG:
+                transpose_r(k - LAG)
+            if k < 16 + MASK_LAG:
+                normalise(k)
+            if LAG <= k and (k - LAG) % TILE_BANKS == TILE_BANKS - 1:
+                quantise_r((k - LAG) // TILE_BANKS)
+
+        for k in range(8):
+            tick(k)
+        wo_codes.append(prepare_weight(wo_raw[2]))
+        for k in range(8, 12):
+            tick(k)
+        for n in range(3):
+            project(0, n)
+        for k in range(12, 16):
+            tick(k)
+        for n in range(3):
+            project(1, n)
+        wo_codes.append(prepare_weight(wo_raw[3]))
+        for k in range(16, 20):
+            tick(k)
+            if k < 19:
+                project(2, k - 16)
+        for i in range(3):
             project(i, 3)
+        for n in range(4):
+            project(3, n)

@@ -90,16 +90,16 @@ def transpose_pass(nc, pools, ident_f32, raw, g, turns):
     return grouped
 
 
-def mx_product(nc, acc, stationary, moving):
+def mx_product(nc, acc, stationary, moving, rows):
     lhs_words, lhs_scales = stationary
     rhs_words, rhs_scales = moving
     for c in range(PASSES):
         nc.tensor.matmul_mx(
-            out=acc[:],
+            out=acc,
             lhsT=lhs_words[:, c, :].bitcast(FP8X4),
             lhsT_scale=lhs_scales[:, c, :],
-            rhs=rhs_words[:, c, :].bitcast(FP8X4),
-            rhs_scale=rhs_scales[:, c, :],
+            rhs=rhs_words[:, c, rows].bitcast(FP8X4),
+            rhs_scale=rhs_scales[:, c, rows],
             start=(c == 0),
             stop=(c == PASSES - 1),
         )
@@ -160,8 +160,13 @@ def tile_differentialattention_pb_kernel(tc, x, diff, Wv, Wo, bo, out):
             quantise_waiting()
             return codes
 
-        wv_raw = [load_rows(wv_rows[0], 4)]
+        first_raw = raw_pool.tile([P, ROW_TILES, WIDTH], BF16, tag="raw")
+        wv_raw = [first_raw]
+        for r in range(2):
+            nc.sync.dma_start(out=first_raw[:, r, :], in_=wv_rows[0][r * P : (r + 1) * P, :])
         x_raw = load_rows(x_rows, 4)
+        for r in range(2, ROW_TILES):
+            nc.sync.dma_start(out=first_raw[:, r, :], in_=wv_rows[0][r * P : (r + 1) * P, :])
         wv_raw.append(load_rows(wv_rows[1], 4))
         half_heads = HEADS // 2
         diff_ga = const.tile([P, GROUP_TOKENS, half_heads * HEADS], BF16)
@@ -231,7 +236,10 @@ def tile_differentialattention_pb_kernel(tc, x, diff, Wv, Wo, bo, out):
 
         def multiply_v(n, i):
             acc = psum.tile([P, CHUNK], F32, tag="bank")
-            mx_product(nc, acc, x_codes[i], wv_codes[n])
+            mx_product(nc, acc[:], x_codes[i], wv_codes[n], slice(0, CHUNK))
+            store_v(n, i, acc)
+
+        def store_v(n, i, acc):
             v_part = staging.tile([P, CHUNK], F32, tag="staging")
             copy_out(
                 nc,
@@ -286,22 +294,39 @@ def tile_differentialattention_pb_kernel(tc, x, diff, Wv, Wo, bo, out):
             )
             v_tiles.append(v_th)
 
-        for r in range(ROW_TILES):
-            prepare_row_tile(0, r)
-        wv_raw.append(load_rows(wv_rows[2], 2))
+        first_accs = []
+
+        def multiply_first(i, half):
+            if half == 0:
+                acc = psum.tile([P, CHUNK], F32, tag="bank")
+                first_accs.append(acc)
+            rows = slice(half * 2 * P, (half + 1) * 2 * P)
+            mx_product(nc, first_accs[i][:, rows], x_codes[i], wv_codes[0], rows)
+            if half == 1:
+                store_v(0, i, first_accs[i])
+
+        prepare_row_tile(0, 0)
+        prepare_row_tile(0, 1)
         prepare_x(0)
         prepare_x(1)
-        multiply_v(0, 0)
         prepare_x(2)
-        multiply_v(0, 1)
+        multiply_first(0, 0)
         prepare_x(3)
-        wv_raw.append(load_rows(wv_rows[3], 2))
+        multiply_first(1, 0)
+        prepare_row_tile(0, 2)
+        multiply_first(2, 0)
+        prepare_row_tile(0, 3)
+        wv_raw.append(load_rows(wv_rows[2], 2))
+        multiply_first(3, 0)
         prepare_row_tile(1, 0)
-        multiply_v(0, 2)
         prepare_row_tile(1, 1)
+        wv_raw.append(load_rows(wv_rows[3], 2))
+        multiply_first(0, 1)
+        multiply_first(1, 1)
         prepare_row_tile(1, 2)
         prepare_row_tile(1, 3)
-        multiply_v(0, 3)
+        multiply_first(2, 1)
+        multiply_first(3, 1)
         wo_raw = [load_rows(wo_rows[0], 2)]
         regroup_mixing_weights()
         multiply_v(1, 0)
@@ -433,17 +458,22 @@ def tile_differentialattention_pb_kernel(tc, x, diff, Wv, Wo, bo, out):
             )
             r_codes.append((r_words, r_scales))
 
-        def project(i, n):
+        def project(i, n, pieces=1):
             tokens = slice(i * P, (i + 1) * P)
-            columns = slice(n * CHUNK, (n + 1) * CHUNK)
             acc = psum.tile([P, CHUNK], F32, tag="bank")
-            mx_product(nc, acc, r_codes[i], wo_codes[n])
             out_part = staging.tile([P, CHUNK], F32, tag="staging")
-            nc.vector.tensor_tensor(out=out_part[:], in0=acc[:], in1=bias[:, columns], op=ALU.add)
-            nc.sync.dma_start(out=out_rows[tokens, columns], in_=out_part[:])
+            width = CHUNK // pieces
+            for piece in range(pieces):
+                part = slice(piece * width, (piece + 1) * width)
+                columns = slice(n * CHUNK + piece * width, n * CHUNK + (piece + 1) * width)
+                mx_product(nc, acc[:, part], r_codes[i], wo_codes[n], part)
+                nc.vector.tensor_tensor(
+                    out=out_part[:, part], in0=acc[:, part], in1=bias[:, columns], op=ALU.add
+                )
+                nc.sync.dma_start(out=out_rows[tokens, columns], in_=out_part[:, part])
 
         LAG = 4
-        MASK_LAG = 2
+        MASK_LAG = 1
 
         def tick(k):
             if k < 16:
@@ -474,4 +504,4 @@ def tile_differentialattention_pb_kernel(tc, x, diff, Wv, Wo, bo, out):
         for i in range(3):
             project(i, 3)
         for n in range(4):
-            project(3, n)
+            project(3, n, 1 if n < 3 else 2)

@@ -109,7 +109,9 @@ def tile_differentialattention_pb_kernel(tc, x, diff, Wv, Wo, bo, out):
     nc = tc.nc
     x_rows = x.flatten_outer_dims()
     out_rows = out.flatten_outer_dims()
-    out_heads = out_rows.rearrange("t (h d) -> (t h) d", h=HEADS)
+    parked_v = out_rows.rearrange("(i n) c -> i (n c)", n=P).rearrange(
+        "i (h n d) -> i h n d", h=HEADS, n=P
+    )
     wv_rows = [Wv[n * CHUNK : (n + 1) * CHUNK, :] for n in range(CHUNKS)]
     wo_rows = [Wo[n * CHUNK : (n + 1) * CHUNK, :] for n in range(CHUNKS)]
 
@@ -160,22 +162,38 @@ def tile_differentialattention_pb_kernel(tc, x, diff, Wv, Wo, bo, out):
             quantise_waiting()
             return codes
 
+        bias_row = const.tile([P, WIDTH], BF16)
+        nc.vector.memset(bias_row[:], 0.0)
+        ones = const.tile([P, P], BF16)
+        nc.gpsimd.memset(ones[:], 1.0)
+        bias = const.tile([P, WIDTH], BF16)
+
+        def spread_bias():
+            for n in range(CHUNKS):
+                columns = slice(n * CHUNK, (n + 1) * CHUNK)
+                spread = psum.tile([P, CHUNK], F32, tag="bank")
+                nc.tensor.matmul(
+                    out=spread[:], lhsT=ones[:], rhs=bias_row[:, columns], start=True, stop=True
+                )
+                copy_out(nc, n, bias[:, columns], spread[:])
+
         first_raw = raw_pool.tile([P, ROW_TILES, WIDTH], BF16, tag="raw")
         wv_raw = [first_raw]
         for r in range(2):
             nc.sync.dma_start(out=first_raw[:, r, :], in_=wv_rows[0][r * P : (r + 1) * P, :])
+        nc.sync.dma_start(out=bias_row[0:1, :], in_=bo.rearrange("(o c) -> o c", o=1))
         x_raw = load_rows(x_rows, 4)
         for r in range(2, ROW_TILES):
             nc.sync.dma_start(out=first_raw[:, r, :], in_=wv_rows[0][r * P : (r + 1) * P, :])
         wv_raw.append(load_rows(wv_rows[1], 4))
         half_heads = HEADS // 2
         diff_ga = const.tile([P, GROUP_TOKENS, half_heads * HEADS], BF16)
-        diff_halves = diff.rearrange("b n a h -> (b n) (a h)").rearrange(
-            "(G t) (s c) -> s G t c", t=GROUP_TOKENS, s=2
+        diff_parts = diff.rearrange("b n a h -> (b n) (a h)").rearrange(
+            "(i t G) (s c) -> i (G s) t c", t=GROUP_TOKENS, G=GROUPS, s=2
         )
-        for s in range(2):
+        for i in range(TOKEN_TILES):
             nc.sync.dma_start(
-                out=diff_ga[s * ALL_GROUPS : (s + 1) * ALL_GROUPS, :, :], in_=diff_halves[s]
+                out=diff_ga[2 * i * GROUPS : 2 * (i + 1) * GROUPS, :, :], in_=diff_parts[i]
             )
 
         ident_f32 = const.tile([P, P], F32)
@@ -185,7 +203,7 @@ def tile_differentialattention_pb_kernel(tc, x, diff, Wv, Wo, bo, out):
         own_token = const.tile([P, GROUP_TOKENS], F32)
         nc.vector.tensor_reduce(
             out=own_token[:],
-            in_=ident_f32[:].rearrange("p (t h) -> p t h", h=HEADS),
+            in_=ident_f32[:].rearrange("p (h t) -> p t h", h=HEADS),
             axis=AXIS.X,
             op=ALU.add,
         )
@@ -248,7 +266,8 @@ def tile_differentialattention_pb_kernel(tc, x, diff, Wv, Wo, bo, out):
                 acc[:].rearrange("p (h w e) -> p h e w", e=2, w=HALF),
             )
             nc.sync.dma_start(
-                out=out_rows[i * P : (i + 1) * P, n * CHUNK : (n + 1) * CHUNK], in_=v_part[:]
+                out=parked_v[i, n * PACK : (n + 1) * PACK].rearrange("h n d -> n h d"),
+                in_=v_part[:].rearrange("p (h d) -> p h d", h=PACK),
             )
 
         mixers = const.tile([P, ALL_GROUPS, P], F32)
@@ -258,21 +277,18 @@ def tile_differentialattention_pb_kernel(tc, x, diff, Wv, Wo, bo, out):
 
         def regroup_mixing_weights():
             nc.scalar.copy(
-                out=diff_la[:].rearrange("p l (t h) -> p l t h", h=HEADS),
-                in_=diff_ga[:].rearrange("p t (l h) -> p l t h", h=HEADS),
+                out=diff_la[:].rearrange("p l (h t) -> p l h t", h=HEADS),
+                in_=diff_ga[:].rearrange("p t (l h) -> p l h t", h=HEADS),
             )
 
         def transpose_mixing_weights():
             diff_th = psum.tile([P, half_heads, P], BF16, tag="bank")
             for l in range(half_heads):
                 nc.tensor.transpose(diff_th[:, l, :], diff_la[:, l, :], ident_bf16[:])
-            for s in range(2):
-                nc.scalar.copy(
-                    out=weights[:, :, s * half_heads : (s + 1) * half_heads],
-                    in_=diff_th[:, :, s * ALL_GROUPS : (s + 1) * ALL_GROUPS].rearrange(
-                        "p l G -> p G l"
-                    ),
-                )
+            nc.scalar.copy(
+                out=weights[:].rearrange("p G (s l) -> p G s l", s=2),
+                in_=diff_th[:].rearrange("p l (G s) -> p G s l", s=2),
+            )
 
         def build_mixer_columns(t):
             nc.scalar.activation(
@@ -288,9 +304,7 @@ def tile_differentialattention_pb_kernel(tc, x, diff, Wv, Wo, bo, out):
             v_th = parked.tile([P, GROUPS, HEAD_COLS], F32, tag="v_th")
             nc.sync.dma_start(
                 out=v_th[:],
-                in_=out_heads[i * P * HEADS : (i + 1) * P * HEADS, :].rearrange(
-                    "(G p) d -> p G d", p=P
-                ),
+                in_=parked_v[i].rearrange("h (t G) d -> (h t) G d", G=GROUPS),
             )
             v_tiles.append(v_th)
 
@@ -333,7 +347,6 @@ def tile_differentialattention_pb_kernel(tc, x, diff, Wv, Wo, bo, out):
         multiply_v(1, 1)
         transpose_mixing_weights()
         wv_codes.append(prepare_weight(wv_raw[2]))
-        wo_raw.append(load_rows(wo_rows[1], 2))
         multiply_v(1, 2)
         build_mixer_columns(0)
         multiply_v(1, 3)
@@ -345,20 +358,23 @@ def tile_differentialattention_pb_kernel(tc, x, diff, Wv, Wo, bo, out):
         build_mixer_columns(3)
         multiply_v(3, 0)
         build_mixer_columns(4)
-        for i in range(1, TOKEN_TILES):
-            if i > 1:
-                multiply_v(2, i)
-            multiply_v(3, i)
-            reload_v(i - 1)
-            if i == 2:
-                wo_raw.append(load_rows(wo_rows[2], 2))
-            build_mixer_columns(4 + i)
+        multiply_v(3, 1)
+        build_mixer_columns(5)
+        multiply_v(2, 2)
+        reload_v(0)
+        multiply_v(3, 2)
+        build_mixer_columns(6)
+        multiply_v(2, 3)
+        multiply_v(3, 3)
+        build_mixer_columns(7)
+        reload_v(1)
+        reload_v(2)
         reload_v(3)
-        bias = const.tile([P, WIDTH], BF16)
-        nc.sync.dma_start(out=bias[:], in_=bo.partition_broadcast(P))
+        wo_raw.append(load_rows(wo_rows[1], 2))
+        wo_raw.append(load_rows(wo_rows[2], 2))
         wo_codes = [prepare_weight(wo_raw[0])]
         wo_raw.append(load_rows(wo_rows[3], 2))
-        wo_codes.append(prepare_weight(wo_raw[1], ((0, 0), (0, 1), (0, 0), (0, 1))))
+        spread_bias()
 
 
         live = {}
@@ -428,24 +444,23 @@ def tile_differentialattention_pb_kernel(tc, x, diff, Wv, Wo, bo, out):
             if b == 0:
                 fresh = grouped_pool.tile([P, CHUNK * PACK], BF16, align_bytes=64, tag="grouped")
                 r_grouped[i] = fresh
-            r_view = r_grouped[i][:].rearrange("p (g x e) -> p g x e", g=PASSES, e=2)
-            run = GROUP_TOKENS * 2
-            bank = psum.tile([P, 2, PASSES, BANK_GROUPS, run], F32, tag="bank")
+            r_view = r_grouped[i][:].rearrange("p (a G u e) -> p a G u e", G=GROUPS, u=2, e=2)
+            bank = psum.tile([P, 2, PASSES, GROUP_TOKENS, BANK_GROUPS, 2], F32, tag="bank")
             for g in range(BANK_GROUPS):
                 for e in range(2):
                     nc.tensor.matmul(
-                        out=bank[:, e, :, g, :],
+                        out=bank[:, e, :, :, g, :],
                         lhsT=live["padded", k][:, 2 * g + e, :, :].rearrange("p s w -> p (s w)"),
                         rhs=pair_sum[:],
                         start=True,
                         stop=True,
                     )
-            first = b * BANK_GROUPS * run
+            in_bank = slice(b * BANK_GROUPS, (b + 1) * BANK_GROUPS)
             copy_out(
                 nc,
                 turn,
-                r_view[:, :, first : first + BANK_GROUPS * run, :],
-                bank[:].rearrange("p e g G x -> p g (G x) e"),
+                r_view[:, :, in_bank, :, :].rearrange("p a G u e -> p a (G u) e"),
+                bank[:].rearrange("p e g t G u -> p (g t) (G u) e"),
             )
 
         def quantise_r(i):
@@ -487,21 +502,25 @@ def tile_differentialattention_pb_kernel(tc, x, diff, Wv, Wo, bo, out):
 
         for k in range(8):
             tick(k)
-        wo_codes.append(prepare_weight(wo_raw[2]))
         for k in range(8, 12):
             tick(k)
-        for n in range(3):
-            project(0, n)
+        project(0, 0)
+        wo_codes.append(prepare_weight(wo_raw[1]))
+        project(1, 0)
         for k in range(12, 16):
             tick(k)
-        for n in range(3):
-            project(1, n)
-        wo_codes.append(prepare_weight(wo_raw[3]))
+        project(0, 1)
+        project(1, 1)
+        wo_codes.append(prepare_weight(wo_raw[2]))
+        project(2, 0)
+        project(2, 1)
         for k in range(16, 20):
             tick(k)
             if k < 19:
-                project(2, k - 16)
+                project(k - 16, 2)
+        wo_codes.append(prepare_weight(wo_raw[3]))
+        for n in range(3):
+            project(3, n)
         for i in range(3):
             project(i, 3)
-        for n in range(4):
-            project(3, n, 1 if n < 3 else 2)
+        project(3, 3, 2)

@@ -168,14 +168,13 @@ def tile_differentialattention_pb_kernel(tc, x, diff, Wv, Wo, bo, out):
         nc.gpsimd.memset(ones[:], 1.0)
         bias = const.tile([P, WIDTH], BF16)
 
-        def spread_bias():
-            for n in range(CHUNKS):
-                columns = slice(n * CHUNK, (n + 1) * CHUNK)
-                spread = psum.tile([P, CHUNK], F32, tag="bank")
-                nc.tensor.matmul(
-                    out=spread[:], lhsT=ones[:], rhs=bias_row[:, columns], start=True, stop=True
-                )
-                copy_out(nc, n, bias[:, columns], spread[:])
+        def spread_bias(n):
+            columns = slice(n * CHUNK, (n + 1) * CHUNK)
+            spread = psum.tile([P, CHUNK], F32, tag="bank")
+            nc.tensor.matmul(
+                out=spread[:], lhsT=ones[:], rhs=bias_row[:, columns], start=True, stop=True
+            )
+            nc.vector.tensor_copy(out=bias[:, columns], in_=spread[:])
 
         first_raw = raw_pool.tile([P, ROW_TILES, WIDTH], BF16, tag="raw")
         wv_raw = [first_raw]
@@ -321,9 +320,13 @@ def tile_differentialattention_pb_kernel(tc, x, diff, Wv, Wo, bo, out):
 
         prepare_row_tile(0, 0)
         prepare_row_tile(0, 1)
+        spread_bias(0)
         prepare_x(0)
+        spread_bias(1)
         prepare_x(1)
+        spread_bias(2)
         prepare_x(2)
+        spread_bias(3)
         multiply_first(0, 0)
         prepare_x(3)
         multiply_first(1, 0)
@@ -349,19 +352,19 @@ def tile_differentialattention_pb_kernel(tc, x, diff, Wv, Wo, bo, out):
         wv_codes.append(prepare_weight(wv_raw[2]))
         multiply_v(1, 2)
         build_mixer_columns(0)
+        wv_codes.append(prepare_weight(wv_raw[3]))
         multiply_v(1, 3)
         build_mixer_columns(1)
-        wv_codes.append(prepare_weight(wv_raw[3]))
         multiply_v(2, 0)
         build_mixer_columns(2)
-        multiply_v(2, 1)
-        build_mixer_columns(3)
         multiply_v(3, 0)
+        build_mixer_columns(3)
+        multiply_v(2, 1)
         build_mixer_columns(4)
         multiply_v(3, 1)
+        reload_v(0)
         build_mixer_columns(5)
         multiply_v(2, 2)
-        reload_v(0)
         multiply_v(3, 2)
         build_mixer_columns(6)
         multiply_v(2, 3)
@@ -374,7 +377,6 @@ def tile_differentialattention_pb_kernel(tc, x, diff, Wv, Wo, bo, out):
         wo_raw.append(load_rows(wo_rows[2], 2))
         wo_codes = [prepare_weight(wo_raw[0])]
         wo_raw.append(load_rows(wo_rows[3], 2))
-        spread_bias()
 
 
         live = {}
@@ -511,14 +513,14 @@ def tile_differentialattention_pb_kernel(tc, x, diff, Wv, Wo, bo, out):
             tick(k)
         project(0, 1)
         project(1, 1)
-        wo_codes.append(prepare_weight(wo_raw[2]))
+        wo_codes.append(prepare_weight(wo_raw[2], ((0, 0), (0, 1), (0, 0), (0, 1))))
         project(2, 0)
         project(2, 1)
         for k in range(16, 20):
             tick(k)
             if k < 19:
                 project(k - 16, 2)
-        wo_codes.append(prepare_weight(wo_raw[3]))
+        wo_codes.append(prepare_weight(wo_raw[3], ((0, 0), (0, 1), (0, 0), (0, 1))))
         for n in range(3):
             project(3, n)
         for i in range(3):

@@ -51,7 +51,7 @@ def copy_out(nc, turn, out, in_):
 
 def transpose_row_tile(nc, pools, ident_f32, raw, r, turns):
     raw_words = raw[:].bitcast(F32)
-    grouped = pools["grouped"].tile([P, CHUNK * PACK], BF16, align_bytes=64, tag="grouped")
+    grouped = pools["grouped"].tile([P, CHUNK * PACK], BF16, align_bytes=256, tag="grouped")
     grouped_words = grouped[:].bitcast(F32).rearrange("p (g r u) -> p g r u", g=PASSES, u=2)
     for half in range(2):
         bank = pools["psum"].tile([P, 4, P], F32, tag="bank")
@@ -69,7 +69,7 @@ def transpose_row_tile(nc, pools, ident_f32, raw, r, turns):
 
 def transpose_pass(nc, pools, ident_f32, raw, g, turns):
     raw_words = raw[:].bitcast(F32)
-    grouped = pools["grouped"].tile([P, CHUNK * PACK], BF16, align_bytes=64, tag="grouped")
+    grouped = pools["grouped"].tile([P, CHUNK * PACK], BF16, align_bytes=256, tag="grouped")
     grouped_words = grouped[:].bitcast(F32).rearrange("p (r u) -> p r u", u=2)
     for half in range(2):
         bank = pools["psum"].tile([P, 2, 2 * P], F32, tag="bank")
@@ -137,8 +137,8 @@ def tile_differentialattention_pb_kernel(tc, x, diff, Wv, Wo, bo, out):
             return raw
 
         def new_codes():
-            words = codes_pool.tile([P, PASSES, CHUNK], U32, align_bytes=64, tag="words")
-            scales = codes_pool.tile([P, PASSES, CHUNK], U8, align_bytes=64, tag="scales")
+            words = codes_pool.tile([P, PASSES, CHUNK], U32, align_bytes=256, tag="words")
+            scales = codes_pool.tile([P, PASSES, CHUNK], U8, align_bytes=256, tag="scales")
             return words, scales
 
         waiting = []
@@ -184,7 +184,7 @@ def tile_differentialattention_pb_kernel(tc, x, diff, Wv, Wo, bo, out):
         x_raw = load_rows(x_rows, 4)
         for r in range(2, ROW_TILES):
             nc.sync.dma_start(out=first_raw[:, r, :], in_=wv_rows[0][r * P : (r + 1) * P, :])
-        wv_raw.append(load_rows(wv_rows[1], 4))
+        wv_raw.append(load_rows(wv_rows[1], 2))
         half_heads = HEADS // 2
         diff_ga = const.tile([P, GROUP_TOKENS, half_heads * HEADS], BF16)
         diff_parts = diff.rearrange("b n a h -> (b n) (a h)").rearrange(
@@ -242,8 +242,8 @@ def tile_differentialattention_pb_kernel(tc, x, diff, Wv, Wo, bo, out):
 
         def prepare_x(i):
             grouped = transpose_row_tile(nc, pools, ident_f32, x_raw, i, RT[2])
-            words = const.tile([P, PASSES, P], U32, align_bytes=64, name="x_words%d" % i)
-            scales = const.tile([P, PASSES, P], U8, align_bytes=64, name="x_scales%d" % i)
+            words = const.tile([P, PASSES, P], U32, align_bytes=256, name="x_words%d" % i)
+            scales = const.tile([P, PASSES, P], U8, align_bytes=256, name="x_scales%d" % i)
             nc.vector.quantize_mx(
                 out=words[:].rearrange("p c k -> p (c k)").bitcast(FP8X4),
                 scales=scales[:].rearrange("p c k -> p (c k)"),
@@ -444,7 +444,7 @@ def tile_differentialattention_pb_kernel(tc, x, diff, Wv, Wo, bo, out):
         def transpose_r(k, turn=0):
             i, b = divmod(k, TILE_BANKS)
             if b == 0:
-                fresh = grouped_pool.tile([P, CHUNK * PACK], BF16, align_bytes=64, tag="grouped")
+                fresh = grouped_pool.tile([P, CHUNK * PACK], BF16, align_bytes=256, tag="grouped")
                 r_grouped[i] = fresh
             r_view = r_grouped[i][:].rearrange("p (a G u e) -> p a G u e", G=GROUPS, u=2, e=2)
             bank = psum.tile([P, 2, PASSES, GROUP_TOKENS, BANK_GROUPS, 2], F32, tag="bank")
@@ -466,8 +466,8 @@ def tile_differentialattention_pb_kernel(tc, x, diff, Wv, Wo, bo, out):
             )
 
         def quantise_r(i):
-            r_words = parked.tile([P, PASSES, P], U32, align_bytes=64)
-            r_scales = parked.tile([P, PASSES, P], U8, align_bytes=64)
+            r_words = parked.tile([P, PASSES, P], U32, align_bytes=256)
+            r_scales = parked.tile([P, PASSES, P], U8, align_bytes=256)
             nc.vector.quantize_mx(
                 out=r_words[:].rearrange("p c k -> p (c k)").bitcast(FP8X4),
                 scales=r_scales[:].rearrange("p c k -> p (c k)"),

import math

import concourse.mybir as mybir
from concourse.masks import make_identity

F32 = mybir.dt.float32
BF16 = mybir.dt.bfloat16
U32 = mybir.dt.uint32
U8 = mybir.dt.uint8
FP8X4 = mybir.dt.float8_e4m3fn_x4
ALU = mybir.AluOpType
ACT = mybir.ActivationFunctionType
AXIS = mybir.AxisListType

P = 128
PACK = 4
K_PASS = P * PACK
TOKENS = 512
WIDTH = 2048
HEADS = 16
HEAD_COLS = WIDTH // HEADS
PASSES = WIDTH // K_PASS
CHUNK = 512
CHUNKS = WIDTH // CHUNK
ROW_TILES = CHUNK // P
TOKEN_TILES = TOKENS // P
GROUP_TOKENS = P // HEADS
GROUPS = P // GROUP_TOKENS
ALL_GROUPS = TOKENS // GROUP_TOKENS
BANK_GROUPS = 4
TILE_BANKS = GROUPS // BANK_GROUPS
HALF = HEAD_COLS // 2
PSUM_BANKS = 8
RT = ((0, 0), (0, 0), (0, 0))
VT = ((1, 1, 1, 1),) + ((0, 1, 0, 1),) * 3
RAW_BUFS = 3

LAMBDA_INIT = 0.8 - 0.6 * math.exp(-0.3 * 12)
KEEP = 1.0 - LAMBDA_INIT
EPS = 1e-5

FLOPS = 2 * 2 * TOKENS * WIDTH * WIDTH + 2 * TOKENS * HEADS * HEADS * HEAD_COLS


def copy_out(nc, turn, out, in_):
    if turn % 2 == 0:
        nc.scalar.copy(out=out, in_=in_)
    else:
        nc.vector.tensor_copy(out=out, in_=in_)


def transpose_row_tile(nc, pools, ident_f32, raw, r, turns):
    raw_words = raw[:].bitcast(F32)
    grouped = pools["grouped"].tile([P, CHUNK * PACK], BF16, align_bytes=256, tag="grouped")
    grouped_words = grouped[:].bitcast(F32).rearrange("p (g r u) -> p g r u", g=PASSES, u=2)
    for half in range(2):
        bank = pools["psum"].tile([P, 4, P], F32, tag="bank")
        for b in range(4):
            first = (4 * half + b) * P
            nc.tensor.transpose(bank[:, b, :], raw_words[:, r, first : first + P], ident_f32[:])
        copy_out(
            nc,
            turns[half],
            grouped_words[:, 2 * half : 2 * half + 2, :, :],
            bank[:].rearrange("p (g u) r -> p g r u", u=2),
        )
    return grouped


def transpose_pass(nc, pools, ident_f32, raw, g, turns):
    raw_words = raw[:].bitcast(F32)
    grouped = pools["grouped"].tile([P, CHUNK * PACK], BF16, align_bytes=256, tag="grouped")
    grouped_words = grouped[:].bitcast(F32).rearrange("p (r u) -> p r u", u=2)
    for half in range(2):
        bank = pools["psum"].tile([P, 2, 2 * P], F32, tag="bank")
        for r in range(2):
            for u in range(2):
                first = (2 * g + u) * P
                nc.tensor.transpose(
                    bank[:, u, r * P : (r + 1) * P],
                    raw_words[:, 2 * half + r, first : first + P],
                    ident_f32[:],
                )
        copy_out(
            nc,
            turns[half],
            grouped_words[:, half * 2 * P : (half + 1) * 2 * P, :],
            bank[:].rearrange("p u r -> p r u"),
        )
    return grouped


def mx_product(nc, acc, stationary, moving, rows):
    lhs_words, lhs_scales = stationary
    rhs_words, rhs_scales = moving
    for c in range(PASSES):
        nc.tensor.matmul_mx(
            out=acc,
            lhsT=lhs_words[:, c, :].bitcast(FP8X4),
            lhsT_scale=lhs_scales[:, c, :],
            rhs=rhs_words[:, c, rows].bitcast(FP8X4),
            rhs_scale=rhs_scales[:, c, rows],
            start=(c == 0),
            stop=(c == PASSES - 1),
        )


def tile_differentialattention_pb_kernel(tc, x, diff, Wv, Wo, bo, out):
    nc = tc.nc
    x_rows = x.flatten_outer_dims()
    out_rows = out.flatten_outer_dims()
    parked_v = out_rows.rearrange("(i n) c -> i (n c)", n=P).rearrange(
        "i (h n d) -> i h n d", h=HEADS, n=P
    )
    wv_rows = [Wv[n * CHUNK : (n + 1) * CHUNK, :] for n in range(CHUNKS)]
    wo_rows = [Wo[n * CHUNK : (n + 1) * CHUNK, :] for n in range(CHUNKS)]

    with (
        tc.tile_pool(name="const", bufs=1) as const,
        tc.tile_pool(name="raw", bufs=RAW_BUFS) as raw_pool,
        tc.tile_pool(name="grouped", bufs=4) as grouped_pool,
        tc.tile_pool(name="codes", bufs=CHUNKS) as codes_pool,
        tc.tile_pool(name="staging", bufs=8) as staging,
        tc.tile_pool(name="mixing", bufs=4) as mixing,
        tc.tile_pool(name="parked", bufs=TOKEN_TILES) as parked,
        tc.psum_pool(name="psum", bufs=PSUM_BANKS) as psum,
        tc.manual_schedule(),
    ):
        pools = {"grouped": grouped_pool, "psum": psum}

        def load_rows(rows, pieces):
            raw = raw_pool.tile([P, ROW_TILES, WIDTH], BF16, tag="raw")
            planes = ROW_TILES // pieces
            by_plane = rows.rearrange("(r p) k -> p r k", p=P)
            for r in range(0, ROW_TILES, planes):
                nc.sync.dma_start(out=raw[:, r : r + planes, :], in_=by_plane[:, r : r + planes, :])
            return raw

        def new_codes():
            words = codes_pool.tile([P, PASSES, CHUNK], U32, align_bytes=256, tag="words")
            scales = codes_pool.tile([P, PASSES, CHUNK], U8, align_bytes=256, tag="scales")
            return words, scales

        waiting = []

        def quantise_waiting():
            if waiting:
                grouped, (words, scales), g = waiting.pop()
                nc.vector.quantize_mx(
                    out=words[:, g, :].bitcast(FP8X4), scales=scales[:, g, :], in_=grouped[:]
                )

        def prepare_pass(raw, codes, g, turns=(0, 1)):
            grouped = transpose_pass(nc, pools, ident_f32, raw, g, turns)
            quantise_waiting()
            waiting.append((grouped, codes, g))

        def prepare_weight(raw, turns=((0, 1),) * PASSES):
            codes = new_codes()
            for g in range(PASSES):
                prepare_pass(raw, codes, g, turns[g])
            quantise_waiting()
            return codes

        bias_row = const.tile([P, WIDTH], BF16)
        nc.vector.memset(bias_row[:], 0.0)
        ones = const.tile([P, P], BF16)
        nc.gpsimd.memset(ones[:], 1.0)
        bias = const.tile([P, WIDTH], BF16)

        def spread_bias(n):
            columns = slice(n * CHUNK, (n + 1) * CHUNK)
            spread = psum.tile([P, CHUNK], F32, tag="bank")
            nc.tensor.matmul(
                out=spread[:], lhsT=ones[:], rhs=bias_row[:, columns], start=True, stop=True
            )
            nc.vector.tensor_copy(out=bias[:, columns], in_=spread[:])

        first_raw = raw_pool.tile([P, ROW_TILES, WIDTH], BF16, tag="raw")
        wv_raw = [first_raw]
        for r in range(2):
            nc.sync.dma_start(out=first_raw[:, r, :], in_=wv_rows[0][r * P : (r + 1) * P, :])
        nc.sync.dma_start(out=bias_row[0:1, :], in_=bo.rearrange("(o c) -> o c", o=1))
        x_raw = load_rows(x_rows, 4)
        for r in range(2, ROW_TILES):
            nc.sync.dma_start(out=first_raw[:, r, :], in_=wv_rows[0][r * P : (r + 1) * P, :])
        wv_raw.append(load_rows(wv_rows[1], 2))
        half_heads = HEADS // 2
        diff_ga = const.tile([P, GROUP_TOKENS, half_heads * HEADS], BF16)
        diff_parts = diff.rearrange("b n a h -> (b n) (a h)").rearrange(
            "(i t G) (s c) -> i (G s) t c", t=GROUP_TOKENS, G=GROUPS, s=2
        )
        for i in range(TOKEN_TILES):
            nc.sync.dma_start(
                out=diff_ga[2 * i * GROUPS : 2 * (i + 1) * GROUPS, :, :], in_=diff_parts[i]
            )

        ident_f32 = const.tile([P, P], F32)
        make_identity(nc, ident_f32[:])
        ident_bf16 = const.tile([P, P], BF16)
        make_identity(nc, ident_bf16[:])
        own_token = const.tile([P, GROUP_TOKENS], F32)
        nc.vector.tensor_reduce(
            out=own_token[:],
            in_=ident_f32[:].rearrange("p (h t) -> p t h", h=HEADS),
            axis=AXIS.X,
            op=ALU.add,
        )
        pair_sum_f32 = const.tile([P, HALF], F32)
        nc.vector.tensor_reduce(
            out=pair_sum_f32[:],
            in_=ident_f32[:].rearrange("p (n s) -> p n s", s=2),
            axis=AXIS.X,
            op=ALU.add,
        )
        pair_sum = const.tile([P, HALF], BF16)
        nc.vector.tensor_copy(out=pair_sum[:], in_=pair_sum_f32[:])
        parity = const.tile([P, 2], F32)
        nc.vector.tensor_reduce(
            out=parity[:],
            in_=ident_f32[:].rearrange("p (n s) -> p s n", s=2),
            axis=AXIS.X,
            op=ALU.add,
        )
        table_warmer = const.tile([P, 1], F32)
        nc.scalar.activation(out=table_warmer[:], in_=own_token[:, 0:1], func=ACT.Sqrt, bias=1.0)

        wv_codes = [new_codes(), new_codes()]

        def prepare_row_tile(n, r):
            words, scales = wv_codes[n]
            grouped = transpose_row_tile(nc, pools, ident_f32, wv_raw[n], r, RT[n])
            rows = slice(r * P, (r + 1) * P)
            for g in range(PASSES):
                nc.vector.quantize_mx(
                    out=words[:, g, rows].bitcast(FP8X4),
                    scales=scales[:, g, rows],
                    in_=grouped[:, g * P * PACK : (g + 1) * P * PACK],
                )

        x_codes = []

        def prepare_x(i):
            grouped = transpose_row_tile(nc, pools, ident_f32, x_raw, i, RT[2])
            words = const.tile([P, PASSES, P], U32, align_bytes=256, name="x_words%d" % i)
            scales = const.tile([P, PASSES, P], U8, align_bytes=256, name="x_scales%d" % i)
            nc.vector.quantize_mx(
                out=words[:].rearrange("p c k -> p (c k)").bitcast(FP8X4),
                scales=scales[:].rearrange("p c k -> p (c k)"),
                in_=grouped[:],
            )
            x_codes.append((words, scales))

        def multiply_v(n, i):
            acc = psum.tile([P, CHUNK], F32, tag="bank")
            mx_product(nc, acc[:], x_codes[i], wv_codes[n], slice(0, CHUNK))
            store_v(n, i, acc)

        def store_v(n, i, acc):
            v_part = staging.tile([P, CHUNK], F32, tag="staging")
            copy_out(
                nc,
                VT[n][i],
                v_part[:].rearrange("p (h e w) -> p h e w", e=2, w=HALF),
                acc[:].rearrange("p (h w e) -> p h e w", e=2, w=HALF),
            )
            nc.sync.dma_start(
                out=parked_v[i, n * PACK : (n + 1) * PACK].rearrange("h n d -> n h d"),
                in_=v_part[:].rearrange("p (h d) -> p h d", h=PACK),
            )

        mixers = const.tile([P, ALL_GROUPS, P], F32)
        mixer_columns = mixers[:].rearrange("p G (g t j) -> p G g t j", g=PASSES, j=PACK)
        weights = const.tile([P, ALL_GROUPS, HEADS], BF16)
        diff_la = const.tile([P, half_heads, P], BF16)

        def regroup_mixing_weights():
            nc.scalar.copy(
                out=diff_la[:].rearrange("p l (h t) -> p l h t", h=HEADS),
                in_=diff_ga[:].rearrange("p t (l h) -> p l h t", h=HEADS),
            )

        def transpose_mixing_weights():
            diff_th = psum.tile([P, half_heads, P], BF16, tag="bank")
            for l in range(half_heads):
                nc.tensor.transpose(diff_th[:, l, :], diff_la[:, l, :], ident_bf16[:])
            nc.scalar.copy(
                out=weights[:].rearrange("p G (s l) -> p G s l", s=2),
                in_=diff_th[:].rearrange("p l (G s) -> p G s l", s=2),
            )

        def build_mixer_columns(t):
            nc.scalar.activation(
                out=mixer_columns[:, :, :, t, :],
                in_=weights[:].rearrange("p G (g j) -> p G g j", j=PACK),
                func=ACT.Copy,
                scale=own_token[:, t : t + 1],
            )

        v_tiles = []

        def reload_v(i):
            v_th = parked.tile([P, GROUPS, HEAD_COLS], F32, tag="v_th")
            nc.sync.dma_start(
                out=v_th[:],
                in_=parked_v[i].rearrange("h (t G) d -> (h t) G d", G=GROUPS),
            )
            v_tiles.append(v_th)

        first_accs = []

        def multiply_first(i, half):
            if half == 0:
                acc = psum.tile([P, CHUNK], F32, tag="bank")
                first_accs.append(acc)
            rows = slice(half * 2 * P, (half + 1) * 2 * P)
            mx_product(nc, first_accs[i][:, rows], x_codes[i], wv_codes[0], rows)
            if half == 1:
                store_v(0, i, first_accs[i])

        prepare_row_tile(0, 0)
        prepare_row_tile(0, 1)
        spread_bias(0)
        prepare_x(0)
        spread_bias(1)
        prepare_x(1)
        spread_bias(2)
        prepare_x(2)
        spread_bias(3)
        multiply_first(0, 0)
        prepare_x(3)
        multiply_first(1, 0)
        prepare_row_tile(0, 2)
        multiply_first(2, 0)
        prepare_row_tile(0, 3)
        wv_raw.append(load_rows(wv_rows[2], 2))
        multiply_first(3, 0)
        prepare_row_tile(1, 0)
        prepare_row_tile(1, 1)
        wv_raw.append(load_rows(wv_rows[3], 2))
        multiply_first(0, 1)
        multiply_first(1, 1)
        prepare_row_tile(1, 2)
        prepare_row_tile(1, 3)
        multiply_first(2, 1)
        multiply_first(3, 1)
        wo_raw = [load_rows(wo_rows[0], 2)]
        regroup_mixing_weights()
        multiply_v(1, 0)
        multiply_v(1, 1)
        transpose_mixing_weights()
        wv_codes.append(prepare_weight(wv_raw[2]))
        multiply_v(1, 2)
        build_mixer_columns(0)
        wv_codes.append(prepare_weight(wv_raw[3]))
        multiply_v(1, 3)
        build_mixer_columns(1)
        multiply_v(2, 0)
        build_mixer_columns(2)
        multiply_v(3, 0)
        build_mixer_columns(3)
        multiply_v(2, 1)
        build_mixer_columns(4)
        multiply_v(3, 1)
        reload_v(0)
        build_mixer_columns(5)
        multiply_v(2, 2)
        multiply_v(3, 2)
        build_mixer_columns(6)
        multiply_v(2, 3)
        multiply_v(3, 3)
        build_mixer_columns(7)
        reload_v(1)
        reload_v(2)
        reload_v(3)
        wo_raw.append(load_rows(wo_rows[1], 2))
        wo_raw.append(load_rows(wo_rows[2], 2))
        wo_codes = [prepare_weight(wo_raw[0])]
        wo_raw.append(load_rows(wo_rows[3], 2))


        live = {}

        def mix(k):
            i, b = divmod(k, TILE_BANKS)
            mixed = psum.tile([P, BANK_GROUPS, HEAD_COLS], F32, tag="bank")
            sum_sq = mixing.tile([P, BANK_GROUPS], F32)
            squares = mixing.tile([P, BANK_GROUPS, HEAD_COLS], BF16)
            for g in range(BANK_GROUPS):
                G = b * BANK_GROUPS + g
                nc.tensor.matmul(
                    out=mixed[:, g, :],
                    lhsT=mixers[:, i * GROUPS + G, :],
                    rhs=v_tiles[i][:, G, :],
                    start=True,
                    stop=True,
                )
            for g in range(BANK_GROUPS):
                nc.scalar.activation(
                    out=squares[:, g, :], in_=mixed[:, g, :], func=ACT.Square, accum_out=sum_sq[:, g : g + 1]
                )
            live["mixed", k] = mixed
            live["sum_sq", k] = sum_sq

        def normalise(k):
            rms = mixing.tile([P, BANK_GROUPS], F32)
            gain = mixing.tile([P, BANK_GROUPS], F32)
            r_bank = mixing.tile([P, BANK_GROUPS, HEAD_COLS], BF16)
            if k < 16:
                nc.scalar.activation(
                    out=rms[:],
                    in_=live["sum_sq", k][:],
                    func=ACT.Sqrt,
                    scale=1.0 / (HEAD_COLS * KEEP * KEEP),
                    bias=EPS / (KEEP * KEEP),
                )
                nc.vector.reciprocal(out=gain[:], in_=rms[:])
            if k >= MASK_LAG:
                pad(k - MASK_LAG)
            if k < 16:
                nc.vector.tensor_tensor(
                    out=r_bank[:],
                    in0=live["mixed", k][:],
                    in1=gain[:].unsqueeze(2).to_broadcast([P, BANK_GROUPS, HEAD_COLS]),
                    op=ALU.mult,
                )
                live["r", k] = r_bank

        def pad(k):
            r_padded = mixing.tile([P, 2 * BANK_GROUPS, 2, HALF], BF16)
            for s in range(2):
                nc.vector.tensor_scalar(
                    out=r_padded[:, :, s, :],
                    in0=live["r", k][:].rearrange("p G (e w) -> p (G e) w", e=2),
                    scalar1=parity[:, s : s + 1],
                    scalar2=None,
                    op0=ALU.mult,
                )
            live["padded", k] = r_padded

        r_grouped = {}
        r_codes = []

        def transpose_r(k, turn=0):
            i, b = divmod(k, TILE_BANKS)
            if b == 0:
                fresh = grouped_pool.tile([P, CHUNK * PACK], BF16, align_bytes=256, tag="grouped")
                r_grouped[i] = fresh
            r_view = r_grouped[i][:].rearrange("p (a G u e) -> p a G u e", G=GROUPS, u=2, e=2)
            bank = psum.tile([P, 2, PASSES, GROUP_TOKENS, BANK_GROUPS, 2], F32, tag="bank")
            for g in range(BANK_GROUPS):
                for e in range(2):
                    nc.tensor.matmul(
                        out=bank[:, e, :, :, g, :],
                        lhsT=live["padded", k][:, 2 * g + e, :, :].rearrange("p s w -> p (s w)"),
                        rhs=pair_sum[:],
                        start=True,
                        stop=True,
                    )
            in_bank = slice(b * BANK_GROUPS, (b + 1) * BANK_GROUPS)
            copy_out(
                nc,
                turn,
                r_view[:, :, in_bank, :, :].rearrange("p a G u e -> p a (G u) e"),
                bank[:].rearrange("p e g t G u -> p (g t) (G u) e"),
            )

        def quantise_r(i):
            r_words = parked.tile([P, PASSES, P], U32, align_bytes=256)
            r_scales = parked.tile([P, PASSES, P], U8, align_bytes=256)
            nc.vector.quantize_mx(
                out=r_words[:].rearrange("p c k -> p (c k)").bitcast(FP8X4),
                scales=r_scales[:].rearrange("p c k -> p (c k)"),
                in_=r_grouped[i][:],
            )
            r_codes.append((r_words, r_scales))

        def project(i, n, pieces=1):
            tokens = slice(i * P, (i + 1) * P)
            acc = psum.tile([P, CHUNK], F32, tag="bank")
            out_part = staging.tile([P, CHUNK], F32, tag="staging")
            width = CHUNK // pieces
            for piece in range(pieces):
                part = slice(piece * width, (piece + 1) * width)
                columns = slice(n * CHUNK + piece * width, n * CHUNK + (piece + 1) * width)
                mx_product(nc, acc[:, part], r_codes[i], wo_codes[n], part)
                nc.vector.tensor_tensor(
                    out=out_part[:, part], in0=acc[:, part], in1=bias[:, columns], op=ALU.add
                )
                nc.sync.dma_start(out=out_rows[tokens, columns], in_=out_part[:, part])

        LAG = 4
        MASK_LAG = 1

        def tick(k):
            if k < 16:
                mix(k)
            if LAG <= k < 16 + LAG:
                transpose_r(k - LAG)
            if k < 16 + MASK_LAG:
                normalise(k)
            if LAG <= k and (k - LAG) % TILE_BANKS == TILE_BANKS - 1:
                quantise_r((k - LAG) // TILE_BANKS)

        for k in range(8):
            tick(k)
        for k in range(8, 12):
            tick(k)
        project(0, 0)
        wo_codes.append(prepare_weight(wo_raw[1]))
        project(1, 0)
        for k in range(12, 16):
            tick(k)
        project(0, 1)
        project(1, 1)
        wo_codes.append(prepare_weight(wo_raw[2], ((0, 0), (0, 1), (0, 0), (0, 1))))
        project(2, 0)
        project(2, 1)
        for k in range(16, 20):
            tick(k)
            if k < 19:
                project(k - 16, 2)
        wo_codes.append(prepare_weight(wo_raw[3], ((0, 0), (0, 1), (0, 0), (0, 1))))
        for n in range(3):
            project(3, n)
        for i in range(3):
            project(i, 3)
        project(3, 3, 2)
